import numpy as np
import ml_dtypes


def mxq(x, axis, fmt="e4m3"):
    dtype, down = {"e4m3": (ml_dtypes.float8_e4m3fn, 7), "e5m2": (ml_dtypes.float8_e5m2, 14)}[fmt]
    v = np.moveaxis(np.asarray(x, np.float32).astype(ml_dtypes.bfloat16).astype(np.float64), axis, -1)
    blocks = v.reshape(v.shape[:-1] + (-1, 32))
    amax = np.abs(blocks).max(-1, keepdims=True)
    byte = np.maximum(np.where(amax > 0, np.frexp(amax)[1] - 1 + 127, 0) - down, 1)
    scale = np.exp2(byte - 127.0)
    codes = (blocks / scale).astype(np.float32).astype(dtype).astype(np.float64)
    return np.moveaxis((codes * scale).reshape(v.shape), -1, axis)


WIDE = False


def mx_kscale(k):
    if not WIDE:
        return np.ones(k)
    levels = np.array([10, -10, 5, -5, 0])
    a = np.random.permutation(np.resize(levels, k // 512 * 4)).reshape(k // 512, 4)
    idx = np.arange(k)
    return np.exp2(a[idx // 512, idx % 128 // 32])


BF16 = ml_dtypes.bfloat16


def bf(x):
    return np.asarray(x, np.float32).astype(BF16)


def f64(x):
    return np.asarray(x).astype(np.float64)


B, L, D, NC, DS = 4, 1024, 512, 1, 1
EPS = 2.0 ** -23


def rmsnorm(v, w):
    ms = np.mean(np.square(v), axis=-1, keepdims=True)
    return v * (1.0 / np.sqrt(ms + EPS)) * w


def setup_inputs():
    s = mx_kscale(D)
    s = s / s.max()
    t = mx_kscale(NC * D)
    tc = t.reshape(NC, D, 1)
    return {"x": bf(np.random.standard_normal((B, L, D)) * s),
            "W_in": bf(np.random.standard_normal((NC * D, D)) / np.sqrt(D) / s[None, :]),
            "W_out": bf(np.random.standard_normal((D, NC * D)) / np.sqrt(NC * D) / t[None, :]),
            "A_theta": bf(np.random.standard_normal((NC, D, DS)) * 0.5),
            "B_real": bf(np.random.standard_normal((NC, D, DS))),
            "B_imag": bf(np.random.standard_normal((NC, D, DS))),
            "C_real": bf(np.random.standard_normal((NC, D, DS)) / np.sqrt(2 * DS) * tc),
            "C_imag": bf(np.random.standard_normal((NC, D, DS)) / np.sqrt(2 * DS) * tc),
            "norm_w": bf(1.0 + 0.1 * np.random.standard_normal(D))}


def reference(x, W_in, W_out, A_theta, B_real, B_imag, C_real, C_imag, norm_w):
    x = f64(x)
    b, l, _ = x.shape
    xi = (mxq(x, 2, "e4m3") @ mxq(f64(W_in), 1, "e4m3").T).reshape(b, l, NC, D)[..., None]
    ct = np.cos(f64(A_theta))
    st = np.sin(f64(A_theta))
    rs = np.zeros((b, l, NC, D, DS))
    is_ = np.zeros_like(rs)
    bxr = f64(B_real) * xi
    bxi = f64(B_imag) * xi
    nr = ct * rs - st * is_ + bxr
    ni = st * rs + ct * is_ + bxi
    y = np.sum(f64(C_real) * nr - f64(C_imag) * ni, axis=-1)
    out = mxq(y.reshape(b, l, NC * D), 2, "e4m3") @ mxq(f64(W_out), 1, "e4m3").T
    return x + rmsnorm(out, f64(norm_w)), nr, ni

@@ -1,0 +1,357 @@
+from contextlib import ExitStack
+
+import concourse.masks as masks
+import concourse.mybir as mybir
+
+F32 = mybir.dt.float32
+BF16 = mybir.dt.bfloat16
+U32 = mybir.dt.uint32
+U8 = mybir.dt.uint8
+FP8X4 = mybir.dt.float8_e4m3fn_x4
+ACT = mybir.ActivationFunctionType
+ALU = mybir.AluOpType
+
+P = 128
+PACK = 4
+D = P * PACK
+TOKENS = 4 * 1024
+GROUP = 512
+TILES = GROUP // P
+N_GROUPS = TOKENS // GROUP
+EPS = 2.0 ** -23
+HALF = GROUP // 2
+RING = 6
+
+FLOPS = 2 * 2 * TOKENS * D * D
+
+ROW_B_REAL = 0
+ROW_B_IMAG = 1
+ROW_C_REAL = 2
+ROW_C_IMAG = 3
+ROW_NORM_W = 4
+
+
+def tile_mamba3core_t_kernel(
+    tc, x, W_in, W_out, A_theta, B_real, B_imag, C_real, C_imag, norm_w, out_0, out_1, out_2
+):
+    nc = tc.nc
+
+    x_groups = x.rearrange("b (h p j) k -> (b h) p j k", p=P, j=TILES)
+    res_groups = out_0.rearrange("b (h p j) k -> (b h) p j k", p=P, j=TILES)
+    nr_groups = out_1.rearrange("b (h p j) c d n -> (b h) p j (c d n)", p=P, j=TILES)
+    ni_groups = out_2.rearrange("b (h p j) c d n -> (b h) p j (c d n)", p=P, j=TILES)
+
+    with ExitStack() as ctx:
+        ctx.enter_context(tc.manual_schedule())
+        consts = ctx.enter_context(tc.tile_pool(name="consts", bufs=1))
+        stage = ctx.enter_context(tc.tile_pool(name="stage", bufs=2))
+        codes = ctx.enter_context(tc.tile_pool(name="codes", bufs=2))
+        results = ctx.enter_context(tc.tile_pool(name="results", bufs=3))
+        small = ctx.enter_context(tc.tile_pool(name="small", bufs=2))
+        psum_vector = ctx.enter_context(tc.psum_pool(name="psum_vector", bufs=2))
+        psum_ring = ctx.enter_context(tc.psum_pool(name="psum_ring", bufs=1))
+        ring_taken = {"count": 0}
+
+        def ring_bank(shape, dtype, name):
+            k = ring_taken["count"]
+            ring_taken["count"] = k + 1
+            return psum_ring.tile(shape, dtype, name=name, tag="ring%d" % (k % RING))
+
+        w_in_sb = consts.tile([P, PACK, D], BF16)
+        w_out_sb = consts.tile([P, PACK, D], BF16)
+        x_sb = [consts.tile([P, TILES, D], BF16, name="x_sb%d" % g) for g in range(N_GROUPS)]
+        nc.sync.dma_start(out=w_in_sb[:], in_=W_in.rearrange("(r p) k -> p r k", p=P))
+        nc.sync.dma_start(out=x_sb[0][:], in_=x_groups[0])
+        nc.sync.dma_start(out=x_sb[1][:], in_=x_groups[1])
+        nc.sync.dma_start(out=w_out_sb[:], in_=W_out.rearrange("(r p) k -> p r k", p=P))
+        for g in range(2, N_GROUPS):
+            nc.sync.dma_start(out=x_sb[g][:], in_=x_groups[g])
+
+        vec_rows = consts.tile([P, D], BF16)
+        nc.vector.memset(vec_rows[:], 0.0)
+        for row, vec in (
+            (ROW_B_REAL, B_real),
+            (ROW_B_IMAG, B_imag),
+            (ROW_C_REAL, C_real),
+            (ROW_C_IMAG, C_imag),
+        ):
+            nc.scalar.dma_start(out=vec_rows[row : row + 1, :], in_=vec.rearrange("c d n -> (c n) d"))
+        nc.scalar.dma_start(
+            out=vec_rows[ROW_NORM_W : ROW_NORM_W + 1, :], in_=norm_w.rearrange("(o d) -> o d", o=1)
+        )
+
+        eps = consts.tile([P, 1], F32)
+        nc.vector.memset(eps[:], EPS)
+        table_warm = consts.tile([P, 1], F32)
+        nc.scalar.activation(out=table_warm[:], in_=eps[:], func=ACT.Sqrt)
+
+        ident_f32 = consts.tile([P, P], F32)
+        masks.make_identity(nc, ident_f32[:])
+        ident_bf16 = consts.tile([P, P], BF16)
+        masks.make_identity(nc, ident_bf16[:])
+
+        def transpose_words(planes, rows_sb, h):
+            for jj in range(2):
+                words = rows_sb[:, 2 * h + jj, :].bitcast(F32)
+                for u in range(2):
+                    nc.tensor.transpose(
+                        planes[:, u, jj * P : (jj + 1) * P], words[:, u * P : (u + 1) * P], ident_f32[:]
+                    )
+
+        def interleave_words(copy, planes, grouped, h):
+            copy(
+                out=grouped[:].bitcast(F32)[:, h * GROUP : (h + 1) * GROUP].rearrange("p (c u) -> p c u", u=2),
+                in_=planes[:].rearrange("p u c -> p c u"),
+            )
+
+        w_in_grouped = consts.tile([P, PACK * D], BF16, align_bytes=64)
+        w_in_codes = consts.tile([P, D], U32, align_bytes=64)
+        w_in_scales = consts.tile([P, D], U8, align_bytes=64)
+        for h in range(2):
+            w_in_planes = psum_vector.tile([P, 2, HALF], F32, tag="bank")
+            transpose_words(w_in_planes, w_in_sb, h)
+            interleave_words(nc.vector.tensor_copy, w_in_planes, w_in_grouped, h)
+        nc.vector.quantize_mx(out=w_in_codes[:].bitcast(FP8X4), scales=w_in_scales[:], in_=w_in_grouped[:])
+
+        x_planes = {}
+        x_grouped = {}
+        x_codes = {}
+        x_scales = {}
+
+        def transpose_x(g):
+            for h in range(2):
+                x_planes[(g, h)] = ring_bank([P, 2, HALF], F32, "x_planes")
+                transpose_words(x_planes[(g, h)], x_sb[g], h)
+
+        def interleave_x(g):
+            x_grouped[g] = stage.tile([P, PACK * GROUP], BF16, align_bytes=64, name="x_grouped", tag="x_grouped")
+            for h in range(2):
+                interleave_words(nc.scalar.copy, x_planes[(g, h)], x_grouped[g], h)
+
+        def quantise_x(g):
+            x_codes[g] = codes.tile([P, GROUP], U32, align_bytes=64, name="x_codes", tag="x_codes")
+            x_scales[g] = codes.tile([P, GROUP], U8, align_bytes=64, name="x_scales", tag="x_scales")
+            nc.vector.quantize_mx(out=x_codes[g][:].bitcast(FP8X4), scales=x_scales[g][:], in_=x_grouped[g][:])
+
+        transpose_x(0)
+        interleave_x(0)
+
+        vec_t = ring_bank([P, PACK, P], BF16, "vec_t")
+        for t in range(PACK):
+            nc.tensor.transpose(vec_t[:, t, :], vec_rows[:, t * P : (t + 1) * P], ident_bf16[:])
+        per_feature = consts.tile([P, PACK, 4], F32)
+        nc.vector.tensor_copy(out=per_feature[:], in_=vec_t[:, :, 0:4])
+        cb_real = consts.tile([P, PACK], F32)
+        cb_imag = consts.tile([P, PACK], F32)
+        gain = consts.tile([P, PACK], F32)
+        nc.vector.tensor_tensor(
+            out=cb_real[:], in0=per_feature[:, :, ROW_C_REAL], in1=per_feature[:, :, ROW_B_REAL], op=ALU.mult
+        )
+        nc.vector.tensor_tensor(
+            out=cb_imag[:], in0=per_feature[:, :, ROW_C_IMAG], in1=per_feature[:, :, ROW_B_IMAG], op=ALU.mult
+        )
+        nc.vector.tensor_tensor(out=gain[:], in0=cb_real[:], in1=cb_imag[:], op=ALU.subtract)
+        quantise_x(0)
+
+        b_real_all = consts.tile([P, D], F32)
+        b_imag_all = consts.tile([P, D], F32)
+        norm_w_all = consts.tile([P, D], F32)
+        for row, spread in ((ROW_B_REAL, b_real_all), (ROW_B_IMAG, b_imag_all), (ROW_NORM_W, norm_w_all)):
+            picked = ring_bank([P, D], F32, "picked")
+            nc.tensor.matmul(
+                picked[:],
+                lhsT=ident_bf16[:, row : row + 1].to_broadcast([P, P]),
+                rhs=vec_rows[:],
+                start=True,
+                stop=True,
+            )
+            nc.scalar.copy(out=spread[:], in_=picked[:])
+
+        transpose_x(1)
+        interleave_x(1)
+
+        w_out_blocks = {}
+        w_out_grouped = consts.tile([P, D, PACK], BF16, align_bytes=64)
+        w_out_codes = consts.tile([P, D], U32, align_bytes=64)
+        w_out_scales = consts.tile([P, D], U8, align_bytes=64)
+
+        def transpose_w_out(r):
+            w_out_blocks[r] = ring_bank([P, PACK, P], BF16, "w_out_blocks")
+            for t in range(PACK):
+                nc.tensor.transpose(w_out_blocks[r][:, t, :], w_out_sb[:, r, t * P : (t + 1) * P], ident_bf16[:])
+
+        def interleave_w_out(r):
+            nc.scalar.copy(
+                out=w_out_grouped[:, r * P : (r + 1) * P, :], in_=w_out_blocks[r][:].rearrange("p t e -> p e t")
+            )
+
+        def quantise_w_out():
+            nc.vector.quantize_mx(
+                out=w_out_codes[:].bitcast(FP8X4),
+                scales=w_out_scales[:],
+                in_=w_out_grouped[:].rearrange("p e t -> p (e t)"),
+            )
+
+        xi_tokens = {}
+        xi_features = {}
+        nr = {}
+        ni = {}
+        y_planes = {}
+        y_grouped = {}
+        y_codes = {}
+        y_scales = {}
+
+        def tokens_pass(g, i):
+            cols = slice(i * P, (i + 1) * P)
+            xi_tokens[(g, i)] = psum_vector.tile([P, D], F32, name="xi_tokens", tag="bank")
+            nc.tensor.matmul_mx(
+                out=xi_tokens[(g, i)][:],
+                lhsT=x_codes[g][:, cols].bitcast(FP8X4),
+                lhsT_scale=x_scales[g][:, cols],
+                rhs=w_in_codes[:].bitcast(FP8X4),
+                rhs_scale=w_in_scales[:],
+                start=True,
+                stop=True,
+            )
+
+        def features_pass(g, t):
+            cols = slice(t * P, (t + 1) * P)
+            xi_features[(g, t)] = ring_bank([P, GROUP], F32, "xi_features")
+            nc.tensor.matmul_mx(
+                out=xi_features[(g, t)][:],
+                lhsT=w_in_codes[:, cols].bitcast(FP8X4),
+                lhsT_scale=w_in_scales[:, cols],
+                rhs=x_codes[g][:].bitcast(FP8X4),
+                rhs_scale=x_scales[g][:],
+                start=True,
+                stop=True,
+            )
+
+        def new_state(g, i):
+            if i == 0:
+                nr[g] = results.tile([P, TILES, D], F32, name="nr", tag="nr")
+                ni[g] = results.tile([P, TILES, D], F32, name="ni", tag="ni")
+            nc.vector.tensor_tensor(out=nr[g][:, i, :], in0=xi_tokens[(g, i)][:], in1=b_real_all[:], op=ALU.mult)
+            nc.vector.tensor_tensor(out=ni[g][:, i, :], in0=xi_tokens[(g, i)][:], in1=b_imag_all[:], op=ALU.mult)
+
+        def scale_y(g):
+            y_planes[g] = stage.tile([P, PACK, GROUP], BF16, name="y_planes", tag="y_planes")
+            for t in range(PACK):
+                nc.scalar.activation(
+                    out=y_planes[g][:, t, :], in_=xi_features[(g, t)][:], func=ACT.Copy, scale=gain[:, t : t + 1]
+                )
+
+        def regroup_y(g):
+            y_grouped[g] = stage.tile([P, GROUP, PACK], BF16, align_bytes=64, name="y_grouped", tag="y_grouped")
+            nc.scalar.copy(
+                out=y_grouped[g][:].rearrange("p (c i) t -> p c t i", i=4),
+                in_=y_planes[g][:].rearrange("p t (c i) -> p c t i", i=4),
+            )
+
+        def quantise_y(g):
+            y_codes[g] = codes.tile([P, GROUP], U32, align_bytes=64, name="y_codes", tag="y_codes")
+            y_scales[g] = codes.tile([P, GROUP], U8, align_bytes=64, name="y_scales", tag="y_scales")
+            nc.vector.quantize_mx(
+                out=y_codes[g][:].bitcast(FP8X4),
+                scales=y_scales[g][:],
+                in_=y_grouped[g][:].rearrange("p c t -> p (c t)"),
+            )
+
+        out_tokens = {}
+        rms = {}
+
+        def out_pass(g, i):
+            cols = slice(i * P, (i + 1) * P)
+            out_tokens[(g, i)] = ring_bank([P, D], F32, "out_tokens")
+            nc.tensor.matmul_mx(
+                out=out_tokens[(g, i)][:],
+                lhsT=y_codes[g][:, cols].bitcast(FP8X4),
+                lhsT_scale=y_scales[g][:, cols],
+                rhs=w_out_codes[:].bitcast(FP8X4),
+                rhs_scale=w_out_scales[:],
+                start=True,
+                stop=True,
+            )
+
+        def root_mean_square(g):
+            squares = stage.tile([P, TILES, D], BF16)
+            sumsq = small.tile([P, TILES], F32)
+            for i in range(TILES):
+                nc.scalar.activation(
+                    out=squares[:, i, :], in_=out_tokens[(g, i)][:], func=ACT.Square, accum_out=sumsq[:, i : i + 1]
+                )
+            rms[g] = small.tile([P, TILES], F32, name="rms", tag="rms")
+            nc.scalar.activation(out=rms[g][:], in_=sumsq[:], func=ACT.Sqrt, scale=1.0 / D, bias=eps[:])
+
+        def finish(g):
+            adder = nc.vector if g == N_GROUPS - 1 else nc.gpsimd
+            res = results.tile([P, TILES, D], F32)
+            rstd = small.tile([P, TILES], F32)
+            nc.vector.reciprocal(out=rstd[:], in_=rms[g][:])
+            for h in range(TILES // 2):
+                pair = slice(2 * h, 2 * h + 2)
+                for i in (2 * h, 2 * h + 1):
+                    nc.vector.scalar_tensor_tensor(
+                        out=res[:, i, :],
+                        in0=out_tokens[(g, i)][:],
+                        scalar=rstd[:, i : i + 1],
+                        in1=norm_w_all[:],
+                        op0=ALU.mult,
+                        op1=ALU.mult,
+                    )
+                adder.tensor_tensor(out=res[:, pair, :], in0=res[:, pair, :], in1=x_sb[g][:, pair, :], op=ALU.add)
+                nc.sync.dma_start(out=res_groups[g][:, pair, :], in_=res[:, pair, :])
+
+        for i in range(2):
+            features_pass(0, i)
+            tokens_pass(0, i)
+        for t in range(2, PACK):
+            features_pass(0, t)
+        for n in range(N_GROUPS + 1):
+            first = n < N_GROUPS
+
+            def second_bank(i):
+                if n == 0:
+                    transpose_w_out(i)
+                else:
+                    out_pass(n - 1, i)
+
+            second_bank(0)
+            second_bank(1)
+            if first:
+                scale_y(n)
+                new_state(n, 0)
+                tokens_pass(n, 2)
+            second_bank(2)
+            second_bank(3)
+            if first:
+                new_state(n, 1)
+                tokens_pass(n, 3)
+            if n + 2 < N_GROUPS:
+                transpose_x(n + 2)
+            if n == 0:
+                for r in range(PACK):
+                    interleave_w_out(r)
+            else:
+                root_mean_square(n - 1)
+            if first:
+                new_state(n, 2)
+                new_state(n, 3)
+                nc.sync.dma_start(out=nr_groups[n], in_=nr[n][:])
+                nc.sync.dma_start(out=ni_groups[n], in_=ni[n][:])
+            if n + 1 < N_GROUPS:
+                quantise_x(n + 1)
+                tokens_pass(n + 1, 0)
+                tokens_pass(n + 1, 1)
+            if n == 0:
+                quantise_w_out()
+            else:
+                finish(n - 1)
+            if n + 1 < N_GROUPS:
+                for t in range(PACK):
+                    features_pass(n + 1, t)
+            if first:
+                regroup_y(n)
+                quantise_y(n)
+            if n + 2 < N_GROUPS:
+                interleave_x(n + 2)

@@ -45,7 +45,7 @@ def tile_mamba3core_t_kernel(
         ctx.enter_context(tc.manual_schedule())
         consts = ctx.enter_context(tc.tile_pool(name="consts", bufs=1))
         stage = ctx.enter_context(tc.tile_pool(name="stage", bufs=2))
-        codes = ctx.enter_context(tc.tile_pool(name="codes", bufs=2))
+        codes = ctx.enter_context(tc.tile_pool(name="codes", bufs=3))
         results = ctx.enter_context(tc.tile_pool(name="results", bufs=3))
         small = ctx.enter_context(tc.tile_pool(name="small", bufs=2))
         psum_vector = ctx.enter_context(tc.psum_pool(name="psum_vector", bufs=2))
@@ -63,8 +63,9 @@ def tile_mamba3core_t_kernel(
         nc.sync.dma_start(out=w_in_sb[:], in_=W_in.rearrange("(r p) k -> p r k", p=P))
         nc.sync.dma_start(out=x_sb[0][:], in_=x_groups[0])
         nc.sync.dma_start(out=x_sb[1][:], in_=x_groups[1])
+        nc.sync.dma_start(out=x_sb[2][:], in_=x_groups[2])
         nc.sync.dma_start(out=w_out_sb[:], in_=W_out.rearrange("(r p) k -> p r k", p=P))
-        for g in range(2, N_GROUPS):
+        for g in range(3, N_GROUPS):
             nc.sync.dma_start(out=x_sb[g][:], in_=x_groups[g])
 
         vec_rows = consts.tile([P, D], BF16)
@@ -135,6 +136,9 @@ def tile_mamba3core_t_kernel(
 
         transpose_x(0)
         interleave_x(0)
+        transpose_x(1)
+        interleave_x(1)
+        quantise_x(0)
 
         vec_t = ring_bank([P, PACK, P], BF16, "vec_t")
         for t in range(PACK):
@@ -151,7 +155,6 @@ def tile_mamba3core_t_kernel(
             out=cb_imag[:], in0=per_feature[:, :, ROW_C_IMAG], in1=per_feature[:, :, ROW_B_IMAG], op=ALU.mult
         )
         nc.vector.tensor_tensor(out=gain[:], in0=cb_real[:], in1=cb_imag[:], op=ALU.subtract)
-        quantise_x(0)
 
         b_real_all = consts.tile([P, D], F32)
         b_imag_all = consts.tile([P, D], F32)
@@ -165,10 +168,7 @@ def tile_mamba3core_t_kernel(
                 start=True,
                 stop=True,
             )
-            nc.scalar.copy(out=spread[:], in_=picked[:])
-
-        transpose_x(1)
-        interleave_x(1)
+            nc.vector.tensor_copy(out=spread[:], in_=picked[:])
 
         w_out_blocks = {}
         w_out_grouped = consts.tile([P, D, PACK], BF16, align_bytes=64)
@@ -283,75 +283,83 @@ def tile_mamba3core_t_kernel(
             rms[g] = small.tile([P, TILES], F32, name="rms", tag="rms")
             nc.scalar.activation(out=rms[g][:], in_=sumsq[:], func=ACT.Sqrt, scale=1.0 / D, bias=eps[:])
 
-        def finish(g):
-            adder = nc.vector if g == N_GROUPS - 1 else nc.gpsimd
-            res = results.tile([P, TILES, D], F32)
-            rstd = small.tile([P, TILES], F32)
-            nc.vector.reciprocal(out=rstd[:], in_=rms[g][:])
-            for h in range(TILES // 2):
-                pair = slice(2 * h, 2 * h + 2)
-                for i in (2 * h, 2 * h + 1):
-                    nc.vector.scalar_tensor_tensor(
-                        out=res[:, i, :],
-                        in0=out_tokens[(g, i)][:],
-                        scalar=rstd[:, i : i + 1],
-                        in1=norm_w_all[:],
-                        op0=ALU.mult,
-                        op1=ALU.mult,
-                    )
-                adder.tensor_tensor(out=res[:, pair, :], in0=res[:, pair, :], in1=x_sb[g][:, pair, :], op=ALU.add)
-                nc.sync.dma_start(out=res_groups[g][:, pair, :], in_=res[:, pair, :])
+        res = {}
+        rstd = {}
 
-        for i in range(2):
-            features_pass(0, i)
-            tokens_pass(0, i)
-        for t in range(2, PACK):
-            features_pass(0, t)
-        for n in range(N_GROUPS + 1):
-            first = n < N_GROUPS
+        def normalise(g, i):
+            if i == 0:
+                res[g] = results.tile([P, TILES, D], F32, name="res", tag="res")
+                rstd[g] = small.tile([P, TILES], F32, name="rstd", tag="rstd")
+                nc.vector.reciprocal(out=rstd[g][:], in_=rms[g][:])
+            nc.vector.scalar_tensor_tensor(
+                out=res[g][:, i, :],
+                in0=out_tokens[(g, i)][:],
+                scalar=rstd[g][:, i : i + 1],
+                in1=norm_w_all[:],
+                op0=ALU.mult,
+                op1=ALU.mult,
+            )
+
+        def add_residual(g, h):
+            adder = nc.vector if g == N_GROUPS - 1 else nc.gpsimd
+            pair = slice(2 * h, 2 * h + 2)
+            adder.tensor_tensor(out=res[g][:, pair, :], in0=res[g][:, pair, :], in1=x_sb[g][:, pair, :], op=ALU.add)
+            nc.sync.dma_start(out=res_groups[g][:, pair, :], in_=res[g][:, pair, :])
+
+        def exists(g):
+            return 0 <= g < N_GROUPS
+
+        for n in range(-1, N_GROUPS + 1):
 
             def second_bank(i):
                 if n == 0:
                     transpose_w_out(i)
-                else:
+                if n >= 1:
                     out_pass(n - 1, i)
 
             second_bank(0)
             second_bank(1)
-            if first:
+            if exists(n):
                 scale_y(n)
                 new_state(n, 0)
                 tokens_pass(n, 2)
             second_bank(2)
             second_bank(3)
-            if first:
+            if exists(n):
                 new_state(n, 1)
                 tokens_pass(n, 3)
-            if n + 2 < N_GROUPS:
-                transpose_x(n + 2)
+            if exists(n + 3):
+                transpose_x(n + 3)
             if n == 0:
                 for r in range(PACK):
                     interleave_w_out(r)
-            else:
+            if n >= 1:
                 root_mean_square(n - 1)
-            if first:
+            if exists(n):
+                regroup_y(n)
+            if exists(n + 3):
+                interleave_x(n + 3)
+            if exists(n):
                 new_state(n, 2)
                 new_state(n, 3)
                 nc.sync.dma_start(out=nr_groups[n], in_=nr[n][:])
                 nc.sync.dma_start(out=ni_groups[n], in_=ni[n][:])
-            if n + 1 < N_GROUPS:
-                quantise_x(n + 1)
+            if exists(n + 1):
                 tokens_pass(n + 1, 0)
                 tokens_pass(n + 1, 1)
+            if n >= 1:
+                for i in range(TILES - 1):
+                    normalise(n - 1, i)
             if n == 0:
                 quantise_w_out()
-            else:
-                finish(n - 1)
-            if n + 1 < N_GROUPS:
+            if exists(n + 2):
+                quantise_x(n + 2)
+            if exists(n):
+                quantise_y(n)
+            if n >= 1:
+                normalise(n - 1, TILES - 1)
+                add_residual(n - 1, 1)
+                add_residual(n - 1, 0)
+            if exists(n + 1):
                 for t in range(PACK):
                     features_pass(n + 1, t)
-            if first:
-                regroup_y(n)
-                quantise_y(n)
-            if n + 2 < N_GROUPS:
-                interleave_x(n + 2)

@@ -49,27 +49,17 @@ def tile_mamba3core_t_kernel(
         results = ctx.enter_context(tc.tile_pool(name="results", bufs=3))
         small = ctx.enter_context(tc.tile_pool(name="small", bufs=2))
         psum_vector = ctx.enter_context(tc.psum_pool(name="psum_vector", bufs=2))
-        psum_ring = ctx.enter_context(tc.psum_pool(name="psum_ring", bufs=1))
-        ring_taken = {"count": 0}
+        psum_out = ctx.enter_context(tc.psum_pool(name="psum_out", bufs=TILES))
+        psum_quick = ctx.enter_context(tc.psum_pool(name="psum_quick", bufs=2))
 
-        def ring_bank(shape, dtype, name):
-            k = ring_taken["count"]
-            ring_taken["count"] = k + 1
-            return psum_ring.tile(shape, dtype, name=name, tag="ring%d" % (k % RING))
+        def quick_bank(shape, dtype, name):
+            return psum_quick.tile(shape, dtype, name=name, tag="quick")
 
-        w_in_sb = consts.tile([P, PACK, D], BF16)
-        w_out_sb = consts.tile([P, PACK, D], BF16)
-        x_sb = [consts.tile([P, TILES, D], BF16, name="x_sb%d" % g) for g in range(N_GROUPS)]
-        nc.sync.dma_start(out=w_in_sb[:], in_=W_in.rearrange("(r p) k -> p r k", p=P))
-        nc.sync.dma_start(out=x_sb[0][:], in_=x_groups[0])
-        nc.sync.dma_start(out=x_sb[1][:], in_=x_groups[1])
-        nc.sync.dma_start(out=x_sb[2][:], in_=x_groups[2])
-        nc.sync.dma_start(out=w_out_sb[:], in_=W_out.rearrange("(r p) k -> p r k", p=P))
-        for g in range(3, N_GROUPS):
-            nc.sync.dma_start(out=x_sb[g][:], in_=x_groups[g])
+        def out_bank(shape, dtype, name):
+            return psum_out.tile(shape, dtype, name=name, tag="out")
 
         vec_rows = consts.tile([P, D], BF16)
-        nc.vector.memset(vec_rows[:], 0.0)
+        nc.gpsimd.memset(vec_rows[:].bitcast(F32), 0.0)
         for row, vec in (
             (ROW_B_REAL, B_real),
             (ROW_B_IMAG, B_imag),
@@ -80,6 +70,19 @@ def tile_mamba3core_t_kernel(
         nc.scalar.dma_start(
             out=vec_rows[ROW_NORM_W : ROW_NORM_W + 1, :], in_=norm_w.rearrange("(o d) -> o d", o=1)
         )
+
+        w_in_sb = consts.tile([P, PACK, D], BF16)
+        w_out_sb = consts.tile([P, PACK, D], BF16)
+        x_sb = [consts.tile([P, TILES, D], BF16, name="x_sb%d" % g) for g in range(N_GROUPS)]
+        w_in_rows = W_in.rearrange("(r p) k -> p r k", p=P)
+        for h in range(2):
+            nc.sync.dma_start(out=w_in_sb[:, 2 * h : 2 * h + 2, :], in_=w_in_rows[:, 2 * h : 2 * h + 2, :])
+        for h in range(2):
+            nc.sync.dma_start(out=x_sb[0][:, 2 * h : 2 * h + 2, :], in_=x_groups[0][:, 2 * h : 2 * h + 2, :])
+        nc.sync.dma_start(out=x_sb[1][:], in_=x_groups[1])
+        nc.sync.dma_start(out=w_out_sb[:], in_=W_out.rearrange("(r p) k -> p r k", p=P))
+        for g in range(2, N_GROUPS):
+            nc.sync.dma_start(out=x_sb[g][:], in_=x_groups[g])
 
         eps = consts.tile([P, 1], F32)
         nc.vector.memset(eps[:], EPS)
@@ -105,62 +108,52 @@ def tile_mamba3core_t_kernel(
                 in_=planes[:].rearrange("p u c -> p c u"),
             )
 
-        w_in_grouped = consts.tile([P, PACK * D], BF16, align_bytes=64)
-        w_in_codes = consts.tile([P, D], U32, align_bytes=64)
-        w_in_scales = consts.tile([P, D], U8, align_bytes=64)
-        for h in range(2):
-            w_in_planes = psum_vector.tile([P, 2, HALF], F32, tag="bank")
-            transpose_words(w_in_planes, w_in_sb, h)
-            interleave_words(nc.vector.tensor_copy, w_in_planes, w_in_grouped, h)
-        nc.vector.quantize_mx(out=w_in_codes[:].bitcast(FP8X4), scales=w_in_scales[:], in_=w_in_grouped[:])
-
         x_planes = {}
         x_grouped = {}
         x_codes = {}
         x_scales = {}
 
-        def transpose_x(g):
-            for h in range(2):
-                x_planes[(g, h)] = ring_bank([P, 2, HALF], F32, "x_planes")
-                transpose_words(x_planes[(g, h)], x_sb[g], h)
+        def transpose_x(g, h):
+            x_planes[(g, h)] = quick_bank([P, 2, HALF], F32, "x_planes")
+            transpose_words(x_planes[(g, h)], x_sb[g], h)
 
-        def interleave_x(g):
-            x_grouped[g] = stage.tile([P, PACK * GROUP], BF16, align_bytes=64, name="x_grouped", tag="x_grouped")
-            for h in range(2):
-                interleave_words(nc.scalar.copy, x_planes[(g, h)], x_grouped[g], h)
+        def interleave_x(g, h):
+            if h == 0:
+                x_grouped[g] = stage.tile(
+                    [P, PACK * GROUP], BF16, align_bytes=64, name="x_grouped", tag="x_grouped"
+                )
+            interleave_words(nc.scalar.copy, x_planes[(g, h)], x_grouped[g], h)
 
-        def quantise_x(g):
-            x_codes[g] = codes.tile([P, GROUP], U32, align_bytes=64, name="x_codes", tag="x_codes")
-            x_scales[g] = codes.tile([P, GROUP], U8, align_bytes=64, name="x_scales", tag="x_scales")
-            nc.vector.quantize_mx(out=x_codes[g][:].bitcast(FP8X4), scales=x_scales[g][:], in_=x_grouped[g][:])
+        def quantise_x(g, tokens):
+            if tokens.start == 0:
+                x_codes[g] = codes.tile([P, GROUP], U32, align_bytes=64, name="x_codes", tag="x_codes")
+                x_scales[g] = codes.tile([P, GROUP], U8, align_bytes=64, name="x_scales", tag="x_scales")
+            nc.vector.quantize_mx(
+                out=x_codes[g][:, tokens].bitcast(FP8X4),
+                scales=x_scales[g][:, tokens],
+                in_=x_grouped[g][:, PACK * tokens.start : PACK * tokens.stop],
+            )
 
-        transpose_x(0)
-        interleave_x(0)
-        transpose_x(1)
-        interleave_x(1)
-        quantise_x(0)
+        WHOLE = slice(0, GROUP)
 
-        vec_t = ring_bank([P, PACK, P], BF16, "vec_t")
-        for t in range(PACK):
-            nc.tensor.transpose(vec_t[:, t, :], vec_rows[:, t * P : (t + 1) * P], ident_bf16[:])
-        per_feature = consts.tile([P, PACK, 4], F32)
-        nc.vector.tensor_copy(out=per_feature[:], in_=vec_t[:, :, 0:4])
-        cb_real = consts.tile([P, PACK], F32)
-        cb_imag = consts.tile([P, PACK], F32)
-        gain = consts.tile([P, PACK], F32)
-        nc.vector.tensor_tensor(
-            out=cb_real[:], in0=per_feature[:, :, ROW_C_REAL], in1=per_feature[:, :, ROW_B_REAL], op=ALU.mult
-        )
-        nc.vector.tensor_tensor(
-            out=cb_imag[:], in0=per_feature[:, :, ROW_C_IMAG], in1=per_feature[:, :, ROW_B_IMAG], op=ALU.mult
-        )
-        nc.vector.tensor_tensor(out=gain[:], in0=cb_real[:], in1=cb_imag[:], op=ALU.subtract)
+        w_in_grouped = consts.tile([P, PACK * D], BF16, align_bytes=64)
+        w_in_codes = consts.tile([P, D], U32, align_bytes=64)
+        w_in_scales = consts.tile([P, D], U8, align_bytes=64)
+        for h, copy in ((0, nc.vector.tensor_copy), (1, nc.scalar.copy)):
+            w_in_planes = psum_vector.tile([P, 2, HALF], F32, tag="bank")
+            transpose_words(w_in_planes, w_in_sb, h)
+            interleave_words(copy, w_in_planes, w_in_grouped, h)
+        nc.vector.quantize_mx(out=w_in_codes[:].bitcast(FP8X4), scales=w_in_scales[:], in_=w_in_grouped[:])
 
-        b_real_all = consts.tile([P, D], F32)
-        b_imag_all = consts.tile([P, D], F32)
+        transpose_x(0, 0)
+        interleave_x(0, 0)
+        quantise_x(0, slice(0, HALF))
+
+        b_all = consts.tile([P, 2, D], F32)
         norm_w_all = consts.tile([P, D], F32)
-        for row, spread in ((ROW_B_REAL, b_real_all), (ROW_B_IMAG, b_imag_all), (ROW_NORM_W, norm_w_all)):
-            picked = ring_bank([P, D], F32, "picked")
+
+        def spread_row(row, copy, out):
+            picked = out_bank([P, D], F32, "picked")
             nc.tensor.matmul(
                 picked[:],
                 lhsT=ident_bf16[:, row : row + 1].to_broadcast([P, P]),
@@ -168,7 +161,28 @@ def tile_mamba3core_t_kernel(
                 start=True,
                 stop=True,
             )
-            nc.vector.tensor_copy(out=spread[:], in_=picked[:])
+            copy(out=out, in_=picked[:])
+
+        spread_row(ROW_B_REAL, nc.vector.tensor_copy, b_all[:, 0, :])
+        spread_row(ROW_B_IMAG, nc.scalar.copy, b_all[:, 1, :])
+        transpose_x(0, 1)
+        interleave_x(0, 1)
+
+        vec_t = out_bank([P, PACK, P], BF16, "vec_t")
+        for t in range(PACK):
+            nc.tensor.transpose(vec_t[:, t, :], vec_rows[:, t * P : (t + 1) * P], ident_bf16[:])
+        per_feature = consts.tile([P, PACK, 4], F32)
+        nc.scalar.copy(out=per_feature[:], in_=vec_t[:, :, 0:4])
+        cb_real = consts.tile([P, PACK], F32)
+        cb_imag = consts.tile([P, PACK], F32)
+        gain = consts.tile([P, PACK], F32)
+        nc.gpsimd.tensor_tensor(
+            out=cb_real[:], in0=per_feature[:, :, ROW_C_REAL], in1=per_feature[:, :, ROW_B_REAL], op=ALU.mult
+        )
+        nc.gpsimd.tensor_tensor(
+            out=cb_imag[:], in0=per_feature[:, :, ROW_C_IMAG], in1=per_feature[:, :, ROW_B_IMAG], op=ALU.mult
+        )
+        nc.gpsimd.tensor_tensor(out=gain[:], in0=cb_real[:], in1=cb_imag[:], op=ALU.subtract)
 
         w_out_blocks = {}
         w_out_grouped = consts.tile([P, D, PACK], BF16, align_bytes=64)
@@ -176,14 +190,12 @@ def tile_mamba3core_t_kernel(
         w_out_scales = consts.tile([P, D], U8, align_bytes=64)
 
         def transpose_w_out(r):
-            w_out_blocks[r] = ring_bank([P, PACK, P], BF16, "w_out_blocks")
+            w_out_blocks[r] = out_bank([P, PACK, P], BF16, "w_out_blocks")
             for t in range(PACK):
                 nc.tensor.transpose(w_out_blocks[r][:, t, :], w_out_sb[:, r, t * P : (t + 1) * P], ident_bf16[:])
 
-        def interleave_w_out(r):
-            nc.scalar.copy(
-                out=w_out_grouped[:, r * P : (r + 1) * P, :], in_=w_out_blocks[r][:].rearrange("p t e -> p e t")
-            )
+        def interleave_w_out(copy, r):
+            copy(out=w_out_grouped[:, r * P : (r + 1) * P, :], in_=w_out_blocks[r][:].rearrange("p t e -> p e t"))
 
         def quantise_w_out():
             nc.vector.quantize_mx(
@@ -194,8 +206,7 @@ def tile_mamba3core_t_kernel(
 
         xi_tokens = {}
         xi_features = {}
-        nr = {}
-        ni = {}
+        state = {}
         y_planes = {}
         y_grouped = {}
         y_codes = {}
@@ -216,7 +227,7 @@ def tile_mamba3core_t_kernel(
 
         def features_pass(g, t):
             cols = slice(t * P, (t + 1) * P)
-            xi_features[(g, t)] = ring_bank([P, GROUP], F32, "xi_features")
+            xi_features[(g, t)] = quick_bank([P, GROUP], F32, "xi_features")
             nc.tensor.matmul_mx(
                 out=xi_features[(g, t)][:],
                 lhsT=w_in_codes[:, cols].bitcast(FP8X4),
@@ -229,10 +240,18 @@ def tile_mamba3core_t_kernel(
 
         def new_state(g, i):
             if i == 0:
-                nr[g] = results.tile([P, TILES, D], F32, name="nr", tag="nr")
-                ni[g] = results.tile([P, TILES, D], F32, name="ni", tag="ni")
-            nc.vector.tensor_tensor(out=nr[g][:, i, :], in0=xi_tokens[(g, i)][:], in1=b_real_all[:], op=ALU.mult)
-            nc.vector.tensor_tensor(out=ni[g][:, i, :], in0=xi_tokens[(g, i)][:], in1=b_imag_all[:], op=ALU.mult)
+                state[g] = results.tile([P, 2, TILES, D], F32, name="state", tag="state")
+            nc.vector.tensor_tensor(
+                out=state[g][:, :, i, :],
+                in0=xi_tokens[(g, i)][:].unsqueeze(1).to_broadcast([P, 2, D]),
+                in1=b_all[:],
+                op=ALU.mult,
+            )
+
+        def store_state(g, h):
+            pair = slice(2 * h, 2 * h + 2)
+            nc.sync.dma_start(out=nr_groups[g][:, pair, :], in_=state[g][:, 0, pair, :])
+            nc.sync.dma_start(out=ni_groups[g][:, pair, :], in_=state[g][:, 1, pair, :])
 
         def scale_y(g):
             y_planes[g] = stage.tile([P, PACK, GROUP], BF16, name="y_planes", tag="y_planes")
@@ -259,10 +278,12 @@ def tile_mamba3core_t_kernel(
 
         out_tokens = {}
         rms = {}
+        rstd = {}
+        res = {}
 
         def out_pass(g, i):
             cols = slice(i * P, (i + 1) * P)
-            out_tokens[(g, i)] = ring_bank([P, D], F32, "out_tokens")
+            out_tokens[(g, i)] = out_bank([P, D], F32, "out_tokens")
             nc.tensor.matmul_mx(
                 out=out_tokens[(g, i)][:],
                 lhsT=y_codes[g][:, cols].bitcast(FP8X4),
@@ -273,93 +294,155 @@ def tile_mamba3core_t_kernel(
                 stop=True,
             )
 
-        def root_mean_square(g):
-            squares = stage.tile([P, TILES, D], BF16)
+        def root_mean_square(g, tiles):
+            squares = stage.tile([P, D], BF16)
             sumsq = small.tile([P, TILES], F32)
-            for i in range(TILES):
+            rms[(g, tiles.start)] = small.tile([P, TILES], F32, name="rms", tag="rms", bufs=4)
+            for i in tiles:
                 nc.scalar.activation(
-                    out=squares[:, i, :], in_=out_tokens[(g, i)][:], func=ACT.Square, accum_out=sumsq[:, i : i + 1]
+                    out=squares[:], in_=out_tokens[(g, i)][:], func=ACT.Square, accum_out=sumsq[:, i : i + 1]
                 )
-            rms[g] = small.tile([P, TILES], F32, name="rms", tag="rms")
-            nc.scalar.activation(out=rms[g][:], in_=sumsq[:], func=ACT.Sqrt, scale=1.0 / D, bias=eps[:])
+            cols = slice(tiles.start, tiles.stop)
+            nc.scalar.activation(
+                out=rms[(g, tiles.start)][:, cols], in_=sumsq[:, cols], func=ACT.Sqrt, scale=1.0 / D, bias=eps[:]
+            )
 
-        res = {}
-        rstd = {}
+        def invert_rms(g, tiles):
+            cols = slice(tiles.start, tiles.stop)
+            inverse = small.tile([P, TILES], F32, name="rstd", tag="rstd", bufs=4)
+            nc.vector.reciprocal(out=inverse[:, cols], in_=rms[(g, tiles.start)][:, cols])
+            for i in tiles:
+                rstd[(g, i)] = inverse[:, i : i + 1]
 
         def normalise(g, i):
-            if i == 0:
+            if g not in res:
                 res[g] = results.tile([P, TILES, D], F32, name="res", tag="res")
-                rstd[g] = small.tile([P, TILES], F32, name="rstd", tag="rstd")
-                nc.vector.reciprocal(out=rstd[g][:], in_=rms[g][:])
             nc.vector.scalar_tensor_tensor(
                 out=res[g][:, i, :],
                 in0=out_tokens[(g, i)][:],
-                scalar=rstd[g][:, i : i + 1],
+                scalar=rstd[(g, i)],
                 in1=norm_w_all[:],
                 op0=ALU.mult,
                 op1=ALU.mult,
             )
 
-        def add_residual(g, h):
-            adder = nc.vector if g == N_GROUPS - 1 else nc.gpsimd
-            pair = slice(2 * h, 2 * h + 2)
-            adder.tensor_tensor(out=res[g][:, pair, :], in0=res[g][:, pair, :], in1=x_sb[g][:, pair, :], op=ALU.add)
-            nc.sync.dma_start(out=res_groups[g][:, pair, :], in_=res[g][:, pair, :])
+        def add_residual(adder, g, first, last):
+            tiles = slice(first, last + 1)
+            adder.tensor_tensor(
+                out=res[g][:, tiles, :], in0=res[g][:, tiles, :], in1=x_sb[g][:, tiles, :], op=ALU.add
+            )
+            nc.sync.dma_start(out=res_groups[g][:, tiles, :], in_=res[g][:, tiles, :])
+
+        ALL = range(TILES)
+        LAST = N_GROUPS - 1
 
         def exists(g):
             return 0 <= g < N_GROUPS
 
-        for n in range(-1, N_GROUPS + 1):
+        tokens_pass(0, 0)
+        tokens_pass(0, 1)
+        new_state(0, 0)
+        quantise_x(0, slice(HALF, GROUP))
+        for h in range(2):
+            transpose_x(1, h)
+            interleave_x(1, h)
+        for t in range(PACK):
+            features_pass(0, t)
+        scale_y(0)
+        new_state(0, 1)
+        store_state(0, 0)
+        tokens_pass(0, 2)
+        tokens_pass(0, 3)
+        quantise_x(1, WHOLE)
+        spread_row(ROW_NORM_W, nc.vector.tensor_copy, norm_w_all[:])
+        for r in range(PACK):
+            transpose_w_out(r)
+        new_state(0, 2)
+        new_state(0, 3)
+        store_state(0, 1)
+        tokens_pass(1, 0)
+        tokens_pass(1, 1)
+        regroup_y(0)
+        for r in range(PACK):
+            interleave_w_out(nc.scalar.copy if r < 2 else nc.vector.tensor_copy, r)
+        quantise_y(0)
+        quantise_w_out()
+        for h in range(2):
+            transpose_x(2, h)
+        for h in range(2):
+            interleave_x(2, h)
+        for t in range(PACK):
+            features_pass(1, t)
+        for i in ALL:
+            out_pass(0, i)
 
-            def second_bank(i):
-                if n == 0:
-                    transpose_w_out(i)
-                if n >= 1:
-                    out_pass(n - 1, i)
-
-            second_bank(0)
-            second_bank(1)
-            if exists(n):
-                scale_y(n)
-                new_state(n, 0)
-                tokens_pass(n, 2)
-            second_bank(2)
-            second_bank(3)
-            if exists(n):
-                new_state(n, 1)
-                tokens_pass(n, 3)
-            if exists(n + 3):
-                transpose_x(n + 3)
-            if n == 0:
-                for r in range(PACK):
-                    interleave_w_out(r)
-            if n >= 1:
-                root_mean_square(n - 1)
-            if exists(n):
-                regroup_y(n)
-            if exists(n + 3):
-                interleave_x(n + 3)
-            if exists(n):
-                new_state(n, 2)
-                new_state(n, 3)
-                nc.sync.dma_start(out=nr_groups[n], in_=nr[n][:])
-                nc.sync.dma_start(out=ni_groups[n], in_=ni[n][:])
-            if exists(n + 1):
-                tokens_pass(n + 1, 0)
-                tokens_pass(n + 1, 1)
-            if n >= 1:
-                for i in range(TILES - 1):
-                    normalise(n - 1, i)
-            if n == 0:
-                quantise_w_out()
+        for n in range(1, LAST):
+            scale_y(n)
+            if n >= 2:
+                invert_rms(n - 2, ALL)
+                for i in range(TILES):
+                    normalise(n - 2, i)
+                add_residual(nc.gpsimd, n - 2, 0, 1)
+                add_residual(nc.gpsimd, n - 2, 2, 3)
+            regroup_y(n)
+            new_state(n, 0)
+            tokens_pass(n, 2)
+            new_state(n, 1)
+            store_state(n, 0)
+            tokens_pass(n, 3)
             if exists(n + 2):
-                quantise_x(n + 2)
-            if exists(n):
-                quantise_y(n)
-            if n >= 1:
-                normalise(n - 1, TILES - 1)
-                add_residual(n - 1, 1)
-                add_residual(n - 1, 0)
-            if exists(n + 1):
-                for t in range(PACK):
-                    features_pass(n + 1, t)
+                for h in range(2):
+                    transpose_x(n + 2, h)
+            root_mean_square(n - 1, ALL)
+            if exists(n + 2):
+                for h in range(2):
+                    interleave_x(n + 2, h)
+            new_state(n, 2)
+            new_state(n, 3)
+            store_state(n, 1)
+            quantise_x(n + 1, WHOLE)
+            tokens_pass(n + 1, 0)
+            tokens_pass(n + 1, 1)
+            for t in range(PACK):
+                features_pass(n + 1, t)
+            quantise_y(n)
+            for i in ALL:
+                out_pass(n, i)
+
+        n = LAST
+        scale_y(n)
+        invert_rms(n - 2, ALL)
+        for i in range(TILES):
+            normalise(n - 2, i)
+        add_residual(nc.gpsimd, n - 2, 0, 1)
+        add_residual(nc.gpsimd, n - 2, 2, 3)
+        regroup_y(n)
+        new_state(n, 0)
+        tokens_pass(n, 2)
+        new_state(n, 1)
+        store_state(n, 0)
+        tokens_pass(n, 3)
+        root_mean_square(n - 1, range(0, 2))
+        root_mean_square(n - 1, range(2, 4))
+        quantise_y(n)
+        invert_rms(n - 1, range(0, 2))
+        normalise(n - 1, 0)
+        normalise(n - 1, 1)
+        add_residual(nc.gpsimd, n - 1, 0, 1)
+        out_pass(n, 0)
+        out_pass(n, 1)
+        new_state(n, 2)
+        new_state(n, 3)
+        store_state(n, 1)
+        invert_rms(n - 1, range(2, 4))
+        normalise(n - 1, 2)
+        normalise(n - 1, 3)
+        add_residual(nc.gpsimd, n - 1, 2, 3)
+        out_pass(n, 2)
+        out_pass(n, 3)
+        for i in ALL:
+            root_mean_square(n, range(i, i + 1))
+        for i in ALL:
+            invert_rms(n, range(i, i + 1))
+            normalise(n, i)
+            add_residual(nc.vector, n, i, i)

@@ -20,7 +20,9 @@ TILES = GROUP // P
 N_GROUPS = TOKENS // GROUP
 EPS = 2.0 ** -23
 HALF = GROUP // 2
-RING = 6
+TOKEN_BANKS = 2
+OUT_BANKS = 3
+QUICK_BANKS = 3
 
 FLOPS = 2 * 2 * TOKENS * D * D
 
@@ -28,7 +30,6 @@ ROW_B_REAL = 0
 ROW_B_IMAG = 1
 ROW_C_REAL = 2
 ROW_C_IMAG = 3
-ROW_NORM_W = 4
 
 
 def tile_mamba3core_t_kernel(
@@ -44,22 +45,32 @@ def tile_mamba3core_t_kernel(
     with ExitStack() as ctx:
         ctx.enter_context(tc.manual_schedule())
         consts = ctx.enter_context(tc.tile_pool(name="consts", bufs=1))
-        stage = ctx.enter_context(tc.tile_pool(name="stage", bufs=2))
-        codes = ctx.enter_context(tc.tile_pool(name="codes", bufs=3))
-        results = ctx.enter_context(tc.tile_pool(name="results", bufs=3))
-        small = ctx.enter_context(tc.tile_pool(name="small", bufs=2))
-        psum_vector = ctx.enter_context(tc.psum_pool(name="psum_vector", bufs=2))
-        psum_out = ctx.enter_context(tc.psum_pool(name="psum_out", bufs=TILES))
-        psum_quick = ctx.enter_context(tc.psum_pool(name="psum_quick", bufs=2))
+        stage = ctx.enter_context(tc.tile_pool(name="stage", bufs=1))
+        codes = ctx.enter_context(tc.tile_pool(name="codes", bufs=1))
+        results = ctx.enter_context(tc.tile_pool(name="results", bufs=1))
+        small = ctx.enter_context(tc.tile_pool(name="small", bufs=1))
+        psum = ctx.enter_context(tc.psum_pool(name="psum", bufs=1))
+        made = {}
 
-        def quick_bank(shape, dtype, name):
-            return psum_quick.tile(shape, dtype, name=name, tag="quick")
+        def rotate(pool, kind, depth, shape, dtype, align_bytes=None):
+            k = made.get(kind, 0)
+            made[kind] = k + 1
+            tag = "%s%d" % (kind, k % depth)
+            return pool.tile(shape, dtype, name=tag, tag=tag, align_bytes=align_bytes)
 
-        def out_bank(shape, dtype, name):
-            return psum_out.tile(shape, dtype, name=name, tag="out")
+        def tokens_bank(shape, dtype):
+            return rotate(psum, "bank_tokens", TOKEN_BANKS, shape, dtype)
+
+        def out_bank(shape, dtype):
+            return rotate(psum, "bank_out", OUT_BANKS, shape, dtype)
+
+        def quick_bank(shape, dtype):
+            return rotate(psum, "bank_quick", QUICK_BANKS, shape, dtype)
 
         vec_rows = consts.tile([P, D], BF16)
         nc.gpsimd.memset(vec_rows[:].bitcast(F32), 0.0)
+        norm_row = consts.tile([P, D], BF16)
+        nc.gpsimd.memset(norm_row[:].bitcast(F32), 0.0)
         for row, vec in (
             (ROW_B_REAL, B_real),
             (ROW_B_IMAG, B_imag),
@@ -67,9 +78,10 @@ def tile_mamba3core_t_kernel(
             (ROW_C_IMAG, C_imag),
         ):
             nc.scalar.dma_start(out=vec_rows[row : row + 1, :], in_=vec.rearrange("c d n -> (c n) d"))
-        nc.scalar.dma_start(
-            out=vec_rows[ROW_NORM_W : ROW_NORM_W + 1, :], in_=norm_w.rearrange("(o d) -> o d", o=1)
-        )
+        eps = consts.tile([P, 1], F32)
+        nc.vector.memset(eps[:], EPS)
+        table_warm = consts.tile([P, 1], F32)
+        nc.scalar.activation(out=table_warm[:], in_=eps[:], func=ACT.Abs_reciprocal_sqrt)
 
         w_in_sb = consts.tile([P, PACK, D], BF16)
         w_out_sb = consts.tile([P, PACK, D], BF16)
@@ -80,14 +92,10 @@ def tile_mamba3core_t_kernel(
         for h in range(2):
             nc.sync.dma_start(out=x_sb[0][:, 2 * h : 2 * h + 2, :], in_=x_groups[0][:, 2 * h : 2 * h + 2, :])
         nc.sync.dma_start(out=x_sb[1][:], in_=x_groups[1])
+        nc.sync.dma_start(out=norm_row[0:1, :], in_=norm_w.rearrange("(o d) -> o d", o=1))
         nc.sync.dma_start(out=w_out_sb[:], in_=W_out.rearrange("(r p) k -> p r k", p=P))
         for g in range(2, N_GROUPS):
             nc.sync.dma_start(out=x_sb[g][:], in_=x_groups[g])
-
-        eps = consts.tile([P, 1], F32)
-        nc.vector.memset(eps[:], EPS)
-        table_warm = consts.tile([P, 1], F32)
-        nc.scalar.activation(out=table_warm[:], in_=eps[:], func=ACT.Sqrt)
 
         ident_f32 = consts.tile([P, P], F32)
         masks.make_identity(nc, ident_f32[:])
@@ -114,20 +122,18 @@ def tile_mamba3core_t_kernel(
         x_scales = {}
 
         def transpose_x(g, h):
-            x_planes[(g, h)] = quick_bank([P, 2, HALF], F32, "x_planes")
+            x_planes[(g, h)] = quick_bank([P, 2, HALF], F32)
             transpose_words(x_planes[(g, h)], x_sb[g], h)
 
         def interleave_x(g, h):
             if h == 0:
-                x_grouped[g] = stage.tile(
-                    [P, PACK * GROUP], BF16, align_bytes=64, name="x_grouped", tag="x_grouped"
-                )
+                x_grouped[g] = rotate(stage, "x_grouped", 2, [P, PACK * GROUP], BF16, 64)
             interleave_words(nc.scalar.copy, x_planes[(g, h)], x_grouped[g], h)
 
         def quantise_x(g, tokens):
             if tokens.start == 0:
-                x_codes[g] = codes.tile([P, GROUP], U32, align_bytes=64, name="x_codes", tag="x_codes")
-                x_scales[g] = codes.tile([P, GROUP], U8, align_bytes=64, name="x_scales", tag="x_scales")
+                x_codes[g] = rotate(codes, "x_codes", 3, [P, GROUP], U32, 64)
+                x_scales[g] = rotate(codes, "x_scales", 3, [P, GROUP], U8, 64)
             nc.vector.quantize_mx(
                 out=x_codes[g][:, tokens].bitcast(FP8X4),
                 scales=x_scales[g][:, tokens],
@@ -140,7 +146,7 @@ def tile_mamba3core_t_kernel(
         w_in_codes = consts.tile([P, D], U32, align_bytes=64)
         w_in_scales = consts.tile([P, D], U8, align_bytes=64)
         for h, copy in ((0, nc.vector.tensor_copy), (1, nc.scalar.copy)):
-            w_in_planes = psum_vector.tile([P, 2, HALF], F32, tag="bank")
+            w_in_planes = tokens_bank([P, 2, HALF], F32)
             transpose_words(w_in_planes, w_in_sb, h)
             interleave_words(copy, w_in_planes, w_in_grouped, h)
         nc.vector.quantize_mx(out=w_in_codes[:].bitcast(FP8X4), scales=w_in_scales[:], in_=w_in_grouped[:])
@@ -152,23 +158,20 @@ def tile_mamba3core_t_kernel(
         b_all = consts.tile([P, 2, D], F32)
         norm_w_all = consts.tile([P, D], F32)
 
-        def spread_row(row, copy, out):
-            picked = out_bank([P, D], F32, "picked")
+        def spread_row(rows, r, copy, out):
+            picked = out_bank([P, D], F32)
             nc.tensor.matmul(
-                picked[:],
-                lhsT=ident_bf16[:, row : row + 1].to_broadcast([P, P]),
-                rhs=vec_rows[:],
-                start=True,
-                stop=True,
+                picked[:], lhsT=ident_bf16[:, r : r + 1].to_broadcast([P, P]), rhs=rows[:], start=True, stop=True
             )
             copy(out=out, in_=picked[:])
 
-        spread_row(ROW_B_REAL, nc.vector.tensor_copy, b_all[:, 0, :])
-        spread_row(ROW_B_IMAG, nc.scalar.copy, b_all[:, 1, :])
+        spread_row(vec_rows, ROW_B_REAL, nc.vector.tensor_copy, b_all[:, 0, :])
+        spread_row(vec_rows, ROW_B_IMAG, nc.scalar.copy, b_all[:, 1, :])
         transpose_x(0, 1)
         interleave_x(0, 1)
+        quantise_x(0, slice(HALF, GROUP))
 
-        vec_t = out_bank([P, PACK, P], BF16, "vec_t")
+        vec_t = out_bank([P, PACK, P], BF16)
         for t in range(PACK):
             nc.tensor.transpose(vec_t[:, t, :], vec_rows[:, t * P : (t + 1) * P], ident_bf16[:])
         per_feature = consts.tile([P, PACK, 4], F32)
@@ -190,7 +193,7 @@ def tile_mamba3core_t_kernel(
         w_out_scales = consts.tile([P, D], U8, align_bytes=64)
 
         def transpose_w_out(r):
-            w_out_blocks[r] = out_bank([P, PACK, P], BF16, "w_out_blocks")
+            w_out_blocks[r] = out_bank([P, PACK, P], BF16)
             for t in range(PACK):
                 nc.tensor.transpose(w_out_blocks[r][:, t, :], w_out_sb[:, r, t * P : (t + 1) * P], ident_bf16[:])
 
@@ -214,7 +217,7 @@ def tile_mamba3core_t_kernel(
 
         def tokens_pass(g, i):
             cols = slice(i * P, (i + 1) * P)
-            xi_tokens[(g, i)] = psum_vector.tile([P, D], F32, name="xi_tokens", tag="bank")
+            xi_tokens[(g, i)] = tokens_bank([P, D], F32)
             nc.tensor.matmul_mx(
                 out=xi_tokens[(g, i)][:],
                 lhsT=x_codes[g][:, cols].bitcast(FP8X4),
@@ -227,7 +230,7 @@ def tile_mamba3core_t_kernel(
 
         def features_pass(g, t):
             cols = slice(t * P, (t + 1) * P)
-            xi_features[(g, t)] = quick_bank([P, GROUP], F32, "xi_features")
+            xi_features[(g, t)] = quick_bank([P, GROUP], F32)
             nc.tensor.matmul_mx(
                 out=xi_features[(g, t)][:],
                 lhsT=w_in_codes[:, cols].bitcast(FP8X4),
@@ -240,7 +243,7 @@ def tile_mamba3core_t_kernel(
 
         def new_state(g, i):
             if i == 0:
-                state[g] = results.tile([P, 2, TILES, D], F32, name="state", tag="state")
+                state[g] = rotate(results, "state", 3, [P, 2, TILES, D], F32)
             nc.vector.tensor_tensor(
                 out=state[g][:, :, i, :],
                 in0=xi_tokens[(g, i)][:].unsqueeze(1).to_broadcast([P, 2, D]),
@@ -253,23 +256,23 @@ def tile_mamba3core_t_kernel(
             nc.sync.dma_start(out=nr_groups[g][:, pair, :], in_=state[g][:, 0, pair, :])
             nc.sync.dma_start(out=ni_groups[g][:, pair, :], in_=state[g][:, 1, pair, :])
 
-        def scale_y(g):
-            y_planes[g] = stage.tile([P, PACK, GROUP], BF16, name="y_planes", tag="y_planes")
-            for t in range(PACK):
-                nc.scalar.activation(
-                    out=y_planes[g][:, t, :], in_=xi_features[(g, t)][:], func=ACT.Copy, scale=gain[:, t : t + 1]
-                )
+        def scale_y(g, t):
+            if t == 0:
+                y_planes[g] = rotate(stage, "y_planes", 2, [P, PACK, GROUP], BF16)
+            nc.scalar.activation(
+                out=y_planes[g][:, t, :], in_=xi_features[(g, t)][:], func=ACT.Copy, scale=gain[:, t : t + 1]
+            )
 
         def regroup_y(g):
-            y_grouped[g] = stage.tile([P, GROUP, PACK], BF16, align_bytes=64, name="y_grouped", tag="y_grouped")
+            y_grouped[g] = rotate(stage, "y_grouped", 2, [P, GROUP, PACK], BF16, 64)
             nc.scalar.copy(
                 out=y_grouped[g][:].rearrange("p (c i) t -> p c t i", i=4),
                 in_=y_planes[g][:].rearrange("p t (c i) -> p c t i", i=4),
             )
 
         def quantise_y(g):
-            y_codes[g] = codes.tile([P, GROUP], U32, align_bytes=64, name="y_codes", tag="y_codes")
-            y_scales[g] = codes.tile([P, GROUP], U8, align_bytes=64, name="y_scales", tag="y_scales")
+            y_codes[g] = rotate(codes, "y_codes", 3, [P, GROUP], U32, 64)
+            y_scales[g] = rotate(codes, "y_scales", 3, [P, GROUP], U8, 64)
             nc.vector.quantize_mx(
                 out=y_codes[g][:].bitcast(FP8X4),
                 scales=y_scales[g][:],
@@ -277,13 +280,12 @@ def tile_mamba3core_t_kernel(
             )
 
         out_tokens = {}
-        rms = {}
         rstd = {}
         res = {}
 
         def out_pass(g, i):
             cols = slice(i * P, (i + 1) * P)
-            out_tokens[(g, i)] = out_bank([P, D], F32, "out_tokens")
+            out_tokens[(g, i)] = out_bank([P, D], F32)
             nc.tensor.matmul_mx(
                 out=out_tokens[(g, i)][:],
                 lhsT=y_codes[g][:, cols].bitcast(FP8X4),
@@ -294,33 +296,34 @@ def tile_mamba3core_t_kernel(
                 stop=True,
             )
 
-        def root_mean_square(g, tiles):
-            squares = stage.tile([P, D], BF16)
-            sumsq = small.tile([P, TILES], F32)
-            rms[(g, tiles.start)] = small.tile([P, TILES], F32, name="rms", tag="rms", bufs=4)
-            for i in tiles:
-                nc.scalar.activation(
-                    out=squares[:], in_=out_tokens[(g, i)][:], func=ACT.Square, accum_out=sumsq[:, i : i + 1]
-                )
-            cols = slice(tiles.start, tiles.stop)
+        sumsq = {}
+
+        def square(g, i):
+            if i == 0:
+                sumsq[g] = rotate(small, "sumsq", 2, [P, TILES], F32)
+                rstd[g] = rotate(small, "rstd", 2, [P, TILES], F32)
+            squares = rotate(stage, "squares", 2, [P, D], BF16)
             nc.scalar.activation(
-                out=rms[(g, tiles.start)][:, cols], in_=sumsq[:, cols], func=ACT.Sqrt, scale=1.0 / D, bias=eps[:]
+                out=squares[:], in_=out_tokens[(g, i)][:], func=ACT.Square, accum_out=sumsq[g][:, i : i + 1]
             )
 
-        def invert_rms(g, tiles):
-            cols = slice(tiles.start, tiles.stop)
-            inverse = small.tile([P, TILES], F32, name="rstd", tag="rstd", bufs=4)
-            nc.vector.reciprocal(out=inverse[:, cols], in_=rms[(g, tiles.start)][:, cols])
-            for i in tiles:
-                rstd[(g, i)] = inverse[:, i : i + 1]
+        def invert_rms(g, first, last):
+            cols = slice(first, last + 1)
+            nc.scalar.activation(
+                out=rstd[g][:, cols],
+                in_=sumsq[g][:, cols],
+                func=ACT.Abs_reciprocal_sqrt,
+                scale=1.0 / D,
+                bias=eps[:],
+            )
 
         def normalise(g, i):
             if g not in res:
-                res[g] = results.tile([P, TILES, D], F32, name="res", tag="res")
+                res[g] = rotate(results, "res", 3, [P, TILES, D], F32)
             nc.vector.scalar_tensor_tensor(
                 out=res[g][:, i, :],
                 in0=out_tokens[(g, i)][:],
-                scalar=rstd[(g, i)],
+                scalar=rstd[g][:, i : i + 1],
                 in1=norm_w_all[:],
                 op0=ALU.mult,
                 op1=ALU.mult,
@@ -331,118 +334,172 @@ def tile_mamba3core_t_kernel(
             adder.tensor_tensor(
                 out=res[g][:, tiles, :], in0=res[g][:, tiles, :], in1=x_sb[g][:, tiles, :], op=ALU.add
             )
+
+        def store_residual(g, first, last):
+            tiles = slice(first, last + 1)
             nc.sync.dma_start(out=res_groups[g][:, tiles, :], in_=res[g][:, tiles, :])
 
-        ALL = range(TILES)
         LAST = N_GROUPS - 1
 
         def exists(g):
             return 0 <= g < N_GROUPS
 
+        transpose_x(1, 0)
+        interleave_x(1, 0)
         tokens_pass(0, 0)
         tokens_pass(0, 1)
-        new_state(0, 0)
-        quantise_x(0, slice(HALF, GROUP))
-        for h in range(2):
-            transpose_x(1, h)
-            interleave_x(1, h)
+        transpose_x(1, 1)
+        interleave_x(1, 1)
         for t in range(PACK):
             features_pass(0, t)
-        scale_y(0)
+        for t in range(PACK):
+            scale_y(0, t)
+        new_state(0, 0)
         new_state(0, 1)
         store_state(0, 0)
         tokens_pass(0, 2)
         tokens_pass(0, 3)
         quantise_x(1, WHOLE)
-        spread_row(ROW_NORM_W, nc.vector.tensor_copy, norm_w_all[:])
+        new_state(0, 2)
+        spread_row(norm_row, 0, nc.vector.tensor_copy, norm_w_all[:])
         for r in range(PACK):
             transpose_w_out(r)
-        new_state(0, 2)
         new_state(0, 3)
         store_state(0, 1)
         tokens_pass(1, 0)
         tokens_pass(1, 1)
+        interleave_w_out(nc.scalar.copy, 0)
+        interleave_w_out(nc.scalar.copy, 1)
+        interleave_w_out(nc.vector.tensor_copy, 2)
+        interleave_w_out(nc.vector.tensor_copy, 3)
         regroup_y(0)
-        for r in range(PACK):
-            interleave_w_out(nc.scalar.copy if r < 2 else nc.vector.tensor_copy, r)
-        quantise_y(0)
-        quantise_w_out()
         for h in range(2):
             transpose_x(2, h)
-        for h in range(2):
             interleave_x(2, h)
-        for t in range(PACK):
-            features_pass(1, t)
-        for i in ALL:
-            out_pass(0, i)
+        quantise_w_out()
+        quantise_y(0)
+        features_pass(1, 0)
+        features_pass(1, 1)
+        transpose_x(3, 0)
+        out_pass(0, 0)
+        out_pass(0, 1)
+        new_state(1, 0)
+        tokens_pass(1, 2)
+        features_pass(1, 2)
+        new_state(1, 1)
+        store_state(1, 0)
+        tokens_pass(1, 3)
+        features_pass(1, 3)
+        out_pass(0, 2)
+        transpose_x(3, 1)
 
         for n in range(1, LAST):
-            scale_y(n)
-            if n >= 2:
-                invert_rms(n - 2, ALL)
-                for i in range(TILES):
-                    normalise(n - 2, i)
-                add_residual(nc.gpsimd, n - 2, 0, 1)
-                add_residual(nc.gpsimd, n - 2, 2, 3)
+            scale_y(n, 0)
+            scale_y(n, 1)
+            if n == 1:
+                interleave_x(3, 0)
+            square(n - 1, 0)
+            scale_y(n, 2)
+            square(n - 1, 1)
+            invert_rms(n - 1, 0, 1)
+            scale_y(n, 3)
+            square(n - 1, 2)
             regroup_y(n)
-            new_state(n, 0)
-            tokens_pass(n, 2)
-            new_state(n, 1)
-            store_state(n, 0)
-            tokens_pass(n, 3)
             if exists(n + 2):
-                for h in range(2):
-                    transpose_x(n + 2, h)
-            root_mean_square(n - 1, ALL)
-            if exists(n + 2):
-                for h in range(2):
-                    interleave_x(n + 2, h)
-            new_state(n, 2)
-            new_state(n, 3)
+                interleave_x(n + 2, 1)
+            if n >= 2:
+                new_state(n, 0)
+                tokens_pass(n, 2)
+            if exists(n + 3):
+                transpose_x(n + 3, 0)
+            if n >= 2:
+                new_state(n, 1)
+                store_state(n, 0)
+                store_residual(n - 2, 2, 3)
+                tokens_pass(n, 3)
+            out_pass(n - 1, 3)
+            if n == 1:
+                quantise_x(2, WHOLE)
+                new_state(n, 2)
+                new_state(n, 3)
+                normalise(n - 1, 0)
+            else:
+                normalise(n - 1, 0)
+                new_state(n, 2)
+                new_state(n, 3)
+            if n >= 2:
+                store_residual(n - 2, 0, 1)
             store_state(n, 1)
-            quantise_x(n + 1, WHOLE)
+            normalise(n - 1, 1)
+            square(n - 1, 3)
+            invert_rms(n - 1, 2, 3)
+            if exists(n + 3):
+                interleave_x(n + 3, 0)
+            quantise_y(n)
+            if exists(n + 2):
+                quantise_x(n + 2, WHOLE)
+            features_pass(n + 1, 0)
             tokens_pass(n + 1, 0)
             tokens_pass(n + 1, 1)
-            for t in range(PACK):
-                features_pass(n + 1, t)
-            quantise_y(n)
-            for i in ALL:
-                out_pass(n, i)
+            features_pass(n + 1, 1)
+            out_pass(n, 0)
+            features_pass(n + 1, 2)
+            out_pass(n, 1)
+            features_pass(n + 1, 3)
+            out_pass(n, 2)
+            if exists(n + 3):
+                transpose_x(n + 3, 1)
+            normalise(n - 1, 2)
+            normalise(n - 1, 3)
+            add_residual(nc.gpsimd, n - 1, 2, 3)
+            add_residual(nc.gpsimd, n - 1, 0, 1)
 
         n = LAST
-        scale_y(n)
-        invert_rms(n - 2, ALL)
-        for i in range(TILES):
-            normalise(n - 2, i)
-        add_residual(nc.gpsimd, n - 2, 0, 1)
-        add_residual(nc.gpsimd, n - 2, 2, 3)
+        scale_y(n, 0)
+        scale_y(n, 1)
+        square(n - 1, 0)
+        scale_y(n, 2)
+        square(n - 1, 1)
+        invert_rms(n - 1, 0, 1)
+        scale_y(n, 3)
         regroup_y(n)
         new_state(n, 0)
         tokens_pass(n, 2)
         new_state(n, 1)
         store_state(n, 0)
+        store_residual(n - 2, 2, 3)
         tokens_pass(n, 3)
-        root_mean_square(n - 1, range(0, 2))
-        root_mean_square(n - 1, range(2, 4))
-        quantise_y(n)
-        invert_rms(n - 1, range(0, 2))
+        out_pass(n - 1, 3)
         normalise(n - 1, 0)
         normalise(n - 1, 1)
         add_residual(nc.gpsimd, n - 1, 0, 1)
-        out_pass(n, 0)
-        out_pass(n, 1)
+        square(n - 1, 2)
+        square(n - 1, 3)
+        invert_rms(n - 1, 2, 3)
         new_state(n, 2)
+        store_residual(n - 2, 0, 1)
         new_state(n, 3)
         store_state(n, 1)
-        invert_rms(n - 1, range(2, 4))
+        quantise_y(n)
+        out_pass(n, 0)
+        out_pass(n, 1)
+        store_residual(n - 1, 0, 1)
         normalise(n - 1, 2)
         normalise(n - 1, 3)
         add_residual(nc.gpsimd, n - 1, 2, 3)
+        store_residual(n - 1, 2, 3)
         out_pass(n, 2)
         out_pass(n, 3)
-        for i in ALL:
-            root_mean_square(n, range(i, i + 1))
-        for i in ALL:
-            invert_rms(n, range(i, i + 1))
-            normalise(n, i)
-            add_residual(nc.vector, n, i, i)
+        for i in range(TILES):
+            square(n, i)
+            invert_rms(n, i, i)
+        normalise(n, 0)
+        normalise(n, 1)
+        normalise(n, 2)
+        add_residual(nc.vector, n, 0, 1)
+        store_residual(n, 0, 1)
+        add_residual(nc.vector, n, 2, 2)
+        store_residual(n, 2, 2)
+        normalise(n, 3)
+        add_residual(nc.vector, n, 3, 3)
+        store_residual(n, 3, 3)

@@ -401,8 +401,8 @@ def tile_mamba3core_t_kernel(
             square(n - 1, 0)
             scale_y(n, 2)
             square(n - 1, 1)
-            invert_rms(n - 1, 0, 1)
             scale_y(n, 3)
+            invert_rms(n - 1, 0, 1)
             square(n - 1, 2)
             regroup_y(n)
             if exists(n + 2):
@@ -432,9 +432,9 @@ def tile_mamba3core_t_kernel(
             store_state(n, 1)
             normalise(n - 1, 1)
             square(n - 1, 3)
-            invert_rms(n - 1, 2, 3)
             if exists(n + 3):
                 interleave_x(n + 3, 0)
+            invert_rms(n - 1, 2, 3)
             quantise_y(n)
             if exists(n + 2):
                 quantise_x(n + 2, WHOLE)
@@ -460,8 +460,8 @@ def tile_mamba3core_t_kernel(
         square(n - 1, 0)
         scale_y(n, 2)
         square(n - 1, 1)
-        invert_rms(n - 1, 0, 1)
         scale_y(n, 3)
+        invert_rms(n - 1, 0, 1)
         regroup_y(n)
         new_state(n, 0)
         tokens_pass(n, 2)

@@ -23,6 +23,8 @@ HALF = GROUP // 2
 TOKEN_BANKS = 2
 OUT_BANKS = 3
 QUICK_BANKS = 3
+SPLIT = 384
+EARLY_SPLIT = 256
 
 FLOPS = 2 * 2 * TOKENS * D * D
 
@@ -263,11 +265,21 @@ def tile_mamba3core_t_kernel(
                 out=y_planes[g][:, t, :], in_=xi_features[(g, t)][:], func=ACT.Copy, scale=gain[:, t : t + 1]
             )
 
-        def regroup_y(g):
+        def regroup_y(g, tokens):
             y_grouped[g] = rotate(stage, "y_grouped", 2, [P, GROUP, PACK], BF16, 64)
             nc.scalar.copy(
-                out=y_grouped[g][:].rearrange("p (c i) t -> p c t i", i=4),
-                in_=y_planes[g][:].rearrange("p t (c i) -> p c t i", i=4),
+                out=y_grouped[g][:, 0:tokens, :].rearrange("p (c i) t -> p c t i", i=4),
+                in_=y_planes[g][:, :, 0:tokens].rearrange("p t (c i) -> p c t i", i=4),
+            )
+
+        def regroup_y_rest(g, tokens):
+            nc.gpsimd.tensor_scalar(
+                out=y_grouped[g][:, tokens:GROUP, :],
+                in0=y_planes[g][:, :, tokens:GROUP].rearrange("p t c -> p c t"),
+                scalar1=1.0,
+                scalar2=0.0,
+                op0=ALU.mult,
+                op1=ALU.add,
             )
 
         def quantise_y(g):
@@ -368,16 +380,17 @@ def tile_mamba3core_t_kernel(
         store_state(0, 1)
         tokens_pass(1, 0)
         tokens_pass(1, 1)
+        regroup_y(0, EARLY_SPLIT)
+        regroup_y_rest(0, EARLY_SPLIT)
         interleave_w_out(nc.scalar.copy, 0)
         interleave_w_out(nc.scalar.copy, 1)
         interleave_w_out(nc.vector.tensor_copy, 2)
         interleave_w_out(nc.vector.tensor_copy, 3)
-        regroup_y(0)
         for h in range(2):
             transpose_x(2, h)
             interleave_x(2, h)
-        quantise_w_out()
         quantise_y(0)
+        quantise_w_out()
         features_pass(1, 0)
         features_pass(1, 1)
         transpose_x(3, 0)
@@ -390,84 +403,87 @@ def tile_mamba3core_t_kernel(
         store_state(1, 0)
         tokens_pass(1, 3)
         features_pass(1, 3)
-        out_pass(0, 2)
         transpose_x(3, 1)
+        out_pass(0, 2)
 
         for n in range(1, LAST):
+            split = EARLY_SPLIT if n == 1 else SPLIT
             scale_y(n, 0)
             scale_y(n, 1)
             if n == 1:
                 interleave_x(3, 0)
-            square(n - 1, 0)
             scale_y(n, 2)
+            square(n - 1, 0)
             square(n - 1, 1)
             scale_y(n, 3)
             invert_rms(n - 1, 0, 1)
             square(n - 1, 2)
-            regroup_y(n)
-            if exists(n + 2):
-                interleave_x(n + 2, 1)
+            regroup_y(n, split)
+            regroup_y_rest(n, split)
             if n >= 2:
                 new_state(n, 0)
                 tokens_pass(n, 2)
-            if exists(n + 3):
-                transpose_x(n + 3, 0)
-            if n >= 2:
                 new_state(n, 1)
                 store_state(n, 0)
-                store_residual(n - 2, 2, 3)
+                add_residual(nc.gpsimd, n - 2, 0, 1)
                 tokens_pass(n, 3)
-            out_pass(n - 1, 3)
+            if exists(n + 3):
+                transpose_x(n + 3, 0)
             if n == 1:
                 quantise_x(2, WHOLE)
                 new_state(n, 2)
                 new_state(n, 3)
+                store_state(n, 1)
                 normalise(n - 1, 0)
+                normalise(n - 1, 1)
             else:
                 normalise(n - 1, 0)
+                normalise(n - 1, 1)
                 new_state(n, 2)
-                new_state(n, 3)
-            if n >= 2:
                 store_residual(n - 2, 0, 1)
-            store_state(n, 1)
-            normalise(n - 1, 1)
+                new_state(n, 3)
+                store_state(n, 1)
+            out_pass(n - 1, 3)
+            if exists(n + 2):
+                interleave_x(n + 2, 1)
             square(n - 1, 3)
             if exists(n + 3):
                 interleave_x(n + 3, 0)
             invert_rms(n - 1, 2, 3)
-            quantise_y(n)
-            if exists(n + 2):
-                quantise_x(n + 2, WHOLE)
             features_pass(n + 1, 0)
-            tokens_pass(n + 1, 0)
-            tokens_pass(n + 1, 1)
             features_pass(n + 1, 1)
-            out_pass(n, 0)
+            tokens_pass(n + 1, 0)
             features_pass(n + 1, 2)
-            out_pass(n, 1)
+            tokens_pass(n + 1, 1)
+            quantise_y(n)
+            out_pass(n, 0)
             features_pass(n + 1, 3)
-            out_pass(n, 2)
+            out_pass(n, 1)
             if exists(n + 3):
                 transpose_x(n + 3, 1)
+            out_pass(n, 2)
             normalise(n - 1, 2)
             normalise(n - 1, 3)
             add_residual(nc.gpsimd, n - 1, 2, 3)
-            add_residual(nc.gpsimd, n - 1, 0, 1)
+            store_residual(n - 1, 2, 3)
+            if exists(n + 2):
+                quantise_x(n + 2, WHOLE)
 
         n = LAST
         scale_y(n, 0)
         scale_y(n, 1)
-        square(n - 1, 0)
         scale_y(n, 2)
+        square(n - 1, 0)
         square(n - 1, 1)
         scale_y(n, 3)
         invert_rms(n - 1, 0, 1)
-        regroup_y(n)
+        regroup_y(n, SPLIT)
+        regroup_y_rest(n, SPLIT)
         new_state(n, 0)
         tokens_pass(n, 2)
         new_state(n, 1)
         store_state(n, 0)
-        store_residual(n - 2, 2, 3)
+        add_residual(nc.gpsimd, n - 2, 0, 1)
         tokens_pass(n, 3)
         out_pass(n - 1, 3)
         normalise(n - 1, 0)

@@ -147,10 +147,10 @@ def tile_mamba3core_t_kernel(
         w_in_grouped = consts.tile([P, PACK * D], BF16, align_bytes=64)
         w_in_codes = consts.tile([P, D], U32, align_bytes=64)
         w_in_scales = consts.tile([P, D], U8, align_bytes=64)
-        for h, copy in ((0, nc.vector.tensor_copy), (1, nc.scalar.copy)):
+        for h in range(2):
             w_in_planes = tokens_bank([P, 2, HALF], F32)
             transpose_words(w_in_planes, w_in_sb, h)
-            interleave_words(copy, w_in_planes, w_in_grouped, h)
+            interleave_words(nc.vector.tensor_copy, w_in_planes, w_in_grouped, h)
         nc.vector.quantize_mx(out=w_in_codes[:].bitcast(FP8X4), scales=w_in_scales[:], in_=w_in_grouped[:])
 
         transpose_x(0, 0)
@@ -160,15 +160,15 @@ def tile_mamba3core_t_kernel(
         b_all = consts.tile([P, 2, D], F32)
         norm_w_all = consts.tile([P, D], F32)
 
-        def spread_row(rows, r, copy, out):
-            picked = out_bank([P, D], F32)
+        def spread_row(bank, rows, r, copy, out):
+            picked = bank([P, D], F32)
             nc.tensor.matmul(
                 picked[:], lhsT=ident_bf16[:, r : r + 1].to_broadcast([P, P]), rhs=rows[:], start=True, stop=True
             )
             copy(out=out, in_=picked[:])
 
-        spread_row(vec_rows, ROW_B_REAL, nc.vector.tensor_copy, b_all[:, 0, :])
-        spread_row(vec_rows, ROW_B_IMAG, nc.scalar.copy, b_all[:, 1, :])
+        spread_row(out_bank, vec_rows, ROW_B_REAL, nc.vector.tensor_copy, b_all[:, 0, :])
+        spread_row(out_bank, vec_rows, ROW_B_IMAG, nc.scalar.copy, b_all[:, 1, :])
         transpose_x(0, 1)
         interleave_x(0, 1)
         quantise_x(0, slice(HALF, GROUP))
@@ -210,6 +210,7 @@ def tile_mamba3core_t_kernel(
             )
 
         xi_tokens = {}
+        xi_copies = {}
         xi_features = {}
         state = {}
         y_planes = {}
@@ -253,6 +254,18 @@ def tile_mamba3core_t_kernel(
                 op=ALU.mult,
             )
 
+        def copy_tokens(g, i):
+            xi_copies[(g, i)] = rotate(stage, "xi_copy", 2, [P, D], F32)
+            nc.scalar.copy(out=xi_copies[(g, i)][:], in_=xi_tokens[(g, i)][:])
+
+        def new_state_from_copy(g, i):
+            nc.gpsimd.tensor_tensor(
+                out=state[g][:, :, i, :],
+                in0=xi_copies[(g, i)][:].unsqueeze(1).to_broadcast([P, 2, D]),
+                in1=b_all[:],
+                op=ALU.mult,
+            )
+
         def store_state(g, h):
             pair = slice(2 * h, 2 * h + 2)
             nc.sync.dma_start(out=nr_groups[g][:, pair, :], in_=state[g][:, 0, pair, :])
@@ -261,12 +274,12 @@ def tile_mamba3core_t_kernel(
         def scale_y(g, t):
             if t == 0:
                 y_planes[g] = rotate(stage, "y_planes", 2, [P, PACK, GROUP], BF16)
+                y_grouped[g] = rotate(stage, "y_grouped", 2, [P, GROUP, PACK], BF16, 64)
             nc.scalar.activation(
                 out=y_planes[g][:, t, :], in_=xi_features[(g, t)][:], func=ACT.Copy, scale=gain[:, t : t + 1]
             )
 
         def regroup_y(g, tokens):
-            y_grouped[g] = rotate(stage, "y_grouped", 2, [P, GROUP, PACK], BF16, 64)
             nc.scalar.copy(
                 out=y_grouped[g][:, 0:tokens, :].rearrange("p (c i) t -> p c t i", i=4),
                 in_=y_planes[g][:, :, 0:tokens].rearrange("p t (c i) -> p c t i", i=4),
@@ -295,9 +308,9 @@ def tile_mamba3core_t_kernel(
         rstd = {}
         res = {}
 
-        def out_pass(g, i):
+        def out_pass(g, i, bank=out_bank):
             cols = slice(i * P, (i + 1) * P)
-            out_tokens[(g, i)] = out_bank([P, D], F32)
+            out_tokens[(g, i)] = bank([P, D], F32)
             nc.tensor.matmul_mx(
                 out=out_tokens[(g, i)][:],
                 lhsT=y_codes[g][:, cols].bitcast(FP8X4),
@@ -366,83 +379,110 @@ def tile_mamba3core_t_kernel(
             features_pass(0, t)
         for t in range(PACK):
             scale_y(0, t)
+        regroup_y_rest(0, 0)
         new_state(0, 0)
         new_state(0, 1)
         store_state(0, 0)
         tokens_pass(0, 2)
         tokens_pass(0, 3)
         quantise_x(1, WHOLE)
-        new_state(0, 2)
-        spread_row(norm_row, 0, nc.vector.tensor_copy, norm_w_all[:])
-        for r in range(PACK):
+        for r in range(3):
             transpose_w_out(r)
-        new_state(0, 3)
-        store_state(0, 1)
-        tokens_pass(1, 0)
-        tokens_pass(1, 1)
-        regroup_y(0, EARLY_SPLIT)
-        regroup_y_rest(0, EARLY_SPLIT)
-        interleave_w_out(nc.scalar.copy, 0)
-        interleave_w_out(nc.scalar.copy, 1)
-        interleave_w_out(nc.vector.tensor_copy, 2)
-        interleave_w_out(nc.vector.tensor_copy, 3)
         for h in range(2):
             transpose_x(2, h)
+        interleave_w_out(nc.scalar.copy, 0)
+        interleave_w_out(nc.scalar.copy, 1)
+        for h in range(2):
             interleave_x(2, h)
-        quantise_y(0)
-        quantise_w_out()
+        new_state(0, 2)
+        interleave_w_out(nc.vector.tensor_copy, 2)
+        tokens_pass(1, 0)
+        transpose_w_out(3)
+        new_state(0, 3)
+        store_state(0, 1)
+        interleave_w_out(nc.vector.tensor_copy, 3)
+        spread_row(quick_bank, norm_row, 0, nc.scalar.copy, norm_w_all[:])
         features_pass(1, 0)
         features_pass(1, 1)
-        transpose_x(3, 0)
+        tokens_pass(1, 1)
+        quantise_w_out()
+        quantise_y(0)
+
+        features_pass(1, 2)
+        features_pass(1, 3)
+        for t in range(PACK):
+            scale_y(1, t)
         out_pass(0, 0)
         out_pass(0, 1)
+        out_pass(0, 2)
+        transpose_x(3, 0)
         new_state(1, 0)
         tokens_pass(1, 2)
-        features_pass(1, 2)
         new_state(1, 1)
         store_state(1, 0)
         tokens_pass(1, 3)
-        features_pass(1, 3)
         transpose_x(3, 1)
-        out_pass(0, 2)
+        square(0, 0)
+        square(0, 1)
+        interleave_x(3, 0)
+        invert_rms(0, 0, 1)
+        square(0, 2)
+        regroup_y(1, EARLY_SPLIT)
+        regroup_y_rest(1, EARLY_SPLIT)
+        quantise_x(2, WHOLE)
+        new_state(1, 2)
+        transpose_x(4, 0)
+        tokens_pass(2, 0)
+        normalise(0, 0)
+        normalise(0, 1)
+        new_state(1, 3)
+        store_state(1, 1)
+        out_pass(0, 3)
+        features_pass(2, 0)
+        features_pass(2, 1)
+        tokens_pass(2, 1)
+        interleave_x(3, 1)
+        square(0, 3)
+        interleave_x(4, 0)
+        invert_rms(0, 2, 3)
+        features_pass(2, 2)
+        quantise_y(1)
+        out_pass(1, 0)
+        features_pass(2, 3)
+        out_pass(1, 1)
+        transpose_x(4, 1)
+        out_pass(1, 2)
+        normalise(0, 2)
+        normalise(0, 3)
+        add_residual(nc.gpsimd, 0, 2, 3)
+        store_residual(0, 2, 3)
+        quantise_x(3, WHOLE)
 
-        for n in range(1, LAST):
-            split = EARLY_SPLIT if n == 1 else SPLIT
+        for n in range(2, LAST):
             scale_y(n, 0)
             scale_y(n, 1)
-            if n == 1:
-                interleave_x(3, 0)
             scale_y(n, 2)
             square(n - 1, 0)
             square(n - 1, 1)
             scale_y(n, 3)
             invert_rms(n - 1, 0, 1)
             square(n - 1, 2)
-            regroup_y(n, split)
-            regroup_y_rest(n, split)
-            if n >= 2:
-                new_state(n, 0)
-                tokens_pass(n, 2)
-                new_state(n, 1)
-                store_state(n, 0)
-                add_residual(nc.gpsimd, n - 2, 0, 1)
-                tokens_pass(n, 3)
+            regroup_y(n, SPLIT)
+            regroup_y_rest(n, SPLIT)
+            new_state(n, 0)
+            tokens_pass(n, 2)
+            new_state(n, 1)
+            store_state(n, 0)
+            add_residual(nc.gpsimd, n - 2, 0, 1)
+            tokens_pass(n, 3)
             if exists(n + 3):
                 transpose_x(n + 3, 0)
-            if n == 1:
-                quantise_x(2, WHOLE)
-                new_state(n, 2)
-                new_state(n, 3)
-                store_state(n, 1)
-                normalise(n - 1, 0)
-                normalise(n - 1, 1)
-            else:
-                normalise(n - 1, 0)
-                normalise(n - 1, 1)
-                new_state(n, 2)
-                store_residual(n - 2, 0, 1)
-                new_state(n, 3)
-                store_state(n, 1)
+            normalise(n - 1, 0)
+            normalise(n - 1, 1)
+            new_state(n, 2)
+            store_residual(n - 2, 0, 1)
+            new_state(n, 3)
+            store_state(n, 1)
             out_pass(n - 1, 3)
             if exists(n + 2):
                 interleave_x(n + 2, 1)
@@ -494,21 +534,21 @@ def tile_mamba3core_t_kernel(
         invert_rms(n - 1, 2, 3)
         new_state(n, 2)
         store_residual(n - 2, 0, 1)
+        quantise_y(n)
+        for i in range(TILES):
+            out_pass(n, i, quick_bank if i < QUICK_BANKS else out_bank)
         new_state(n, 3)
         store_state(n, 1)
-        quantise_y(n)
-        out_pass(n, 0)
-        out_pass(n, 1)
         store_residual(n - 1, 0, 1)
         normalise(n - 1, 2)
         normalise(n - 1, 3)
         add_residual(nc.gpsimd, n - 1, 2, 3)
         store_residual(n - 1, 2, 3)
-        out_pass(n, 2)
-        out_pass(n, 3)
-        for i in range(TILES):
+        square(n, 0)
+        for i in range(1, TILES):
             square(n, i)
-            invert_rms(n, i, i)
+            invert_rms(n, i - 1, i - 1)
+        invert_rms(n, TILES - 1, TILES - 1)
         normalise(n, 0)
         normalise(n, 1)
         normalise(n, 2)

@@ -23,8 +23,12 @@ HALF = GROUP // 2
 TOKEN_BANKS = 2
 OUT_BANKS = 3
 QUICK_BANKS = 3
+WHOLE = slice(0, GROUP)
+FIRST_HALF = slice(0, HALF)
+SECOND_HALF = slice(HALF, GROUP)
 SPLIT = 384
-EARLY_SPLIT = 256
+FOR_SCALAR = slice(0, SPLIT)
+FOR_GPSIMD = slice(SPLIT, GROUP)
 
 FLOPS = 2 * 2 * TOKENS * D * D
 
@@ -142,8 +146,6 @@ def tile_mamba3core_t_kernel(
                 in_=x_grouped[g][:, PACK * tokens.start : PACK * tokens.stop],
             )
 
-        WHOLE = slice(0, GROUP)
-
         w_in_grouped = consts.tile([P, PACK * D], BF16, align_bytes=64)
         w_in_codes = consts.tile([P, D], U32, align_bytes=64)
         w_in_scales = consts.tile([P, D], U8, align_bytes=64)
@@ -155,7 +157,7 @@ def tile_mamba3core_t_kernel(
 
         transpose_x(0, 0)
         interleave_x(0, 0)
-        quantise_x(0, slice(0, HALF))
+        quantise_x(0, FIRST_HALF)
 
         b_all = consts.tile([P, 2, D], F32)
         norm_w_all = consts.tile([P, D], F32)
@@ -171,7 +173,7 @@ def tile_mamba3core_t_kernel(
         spread_row(out_bank, vec_rows, ROW_B_IMAG, nc.scalar.copy, b_all[:, 1, :])
         transpose_x(0, 1)
         interleave_x(0, 1)
-        quantise_x(0, slice(HALF, GROUP))
+        quantise_x(0, SECOND_HALF)
 
         vec_t = out_bank([P, PACK, P], BF16)
         for t in range(PACK):
@@ -281,27 +283,28 @@ def tile_mamba3core_t_kernel(
 
         def regroup_y(g, tokens):
             nc.scalar.copy(
-                out=y_grouped[g][:, 0:tokens, :].rearrange("p (c i) t -> p c t i", i=4),
-                in_=y_planes[g][:, :, 0:tokens].rearrange("p t (c i) -> p c t i", i=4),
+                out=y_grouped[g][:, tokens, :].rearrange("p (c i) t -> p c t i", i=4),
+                in_=y_planes[g][:, :, tokens].rearrange("p t (c i) -> p c t i", i=4),
             )
 
-        def regroup_y_rest(g, tokens):
+        def regroup_y_gpsimd(g, tokens):
             nc.gpsimd.tensor_scalar(
-                out=y_grouped[g][:, tokens:GROUP, :],
-                in0=y_planes[g][:, :, tokens:GROUP].rearrange("p t c -> p c t"),
+                out=y_grouped[g][:, tokens, :],
+                in0=y_planes[g][:, :, tokens].rearrange("p t c -> p c t"),
                 scalar1=1.0,
                 scalar2=0.0,
                 op0=ALU.mult,
                 op1=ALU.add,
             )
 
-        def quantise_y(g):
-            y_codes[g] = rotate(codes, "y_codes", 3, [P, GROUP], U32, 64)
-            y_scales[g] = rotate(codes, "y_scales", 3, [P, GROUP], U8, 64)
+        def quantise_y(g, tokens):
+            if tokens.start == 0:
+                y_codes[g] = rotate(codes, "y_codes", 3, [P, GROUP], U32, 64)
+                y_scales[g] = rotate(codes, "y_scales", 3, [P, GROUP], U8, 64)
             nc.vector.quantize_mx(
-                out=y_codes[g][:].bitcast(FP8X4),
-                scales=y_scales[g][:],
-                in_=y_grouped[g][:].rearrange("p c t -> p (c t)"),
+                out=y_codes[g][:, tokens].bitcast(FP8X4),
+                scales=y_scales[g][:, tokens],
+                in_=y_grouped[g][:, tokens, :].rearrange("p c t -> p (c t)"),
             )
 
         out_tokens = {}
@@ -375,15 +378,16 @@ def tile_mamba3core_t_kernel(
         tokens_pass(0, 1)
         transpose_x(1, 1)
         interleave_x(1, 1)
-        for t in range(PACK):
+        for t in range(3):
             features_pass(0, t)
+        new_state(0, 0)
+        tokens_pass(0, 2)
+        features_pass(0, 3)
         for t in range(PACK):
             scale_y(0, t)
-        regroup_y_rest(0, 0)
-        new_state(0, 0)
+        regroup_y_gpsimd(0, WHOLE)
         new_state(0, 1)
         store_state(0, 0)
-        tokens_pass(0, 2)
         tokens_pass(0, 3)
         quantise_x(1, WHOLE)
         for r in range(3):
@@ -406,7 +410,7 @@ def tile_mamba3core_t_kernel(
         features_pass(1, 1)
         tokens_pass(1, 1)
         quantise_w_out()
-        quantise_y(0)
+        quantise_y(0, WHOLE)
 
         features_pass(1, 2)
         features_pass(1, 3)
@@ -427,10 +431,10 @@ def tile_mamba3core_t_kernel(
         interleave_x(3, 0)
         invert_rms(0, 0, 1)
         square(0, 2)
-        regroup_y(1, EARLY_SPLIT)
-        regroup_y_rest(1, EARLY_SPLIT)
-        quantise_x(2, WHOLE)
+        regroup_y(1, FIRST_HALF)
+        regroup_y_gpsimd(1, SECOND_HALF)
         new_state(1, 2)
+        quantise_x(2, WHOLE)
         transpose_x(4, 0)
         tokens_pass(2, 0)
         normalise(0, 0)
@@ -446,7 +450,7 @@ def tile_mamba3core_t_kernel(
         interleave_x(4, 0)
         invert_rms(0, 2, 3)
         features_pass(2, 2)
-        quantise_y(1)
+        quantise_y(1, WHOLE)
         out_pass(1, 0)
         features_pass(2, 3)
         out_pass(1, 1)
@@ -467,8 +471,8 @@ def tile_mamba3core_t_kernel(
             scale_y(n, 3)
             invert_rms(n - 1, 0, 1)
             square(n - 1, 2)
-            regroup_y(n, SPLIT)
-            regroup_y_rest(n, SPLIT)
+            regroup_y(n, FOR_SCALAR)
+            regroup_y_gpsimd(n, FOR_GPSIMD)
             new_state(n, 0)
             tokens_pass(n, 2)
             new_state(n, 1)
@@ -495,7 +499,7 @@ def tile_mamba3core_t_kernel(
             tokens_pass(n + 1, 0)
             features_pass(n + 1, 2)
             tokens_pass(n + 1, 1)
-            quantise_y(n)
+            quantise_y(n, WHOLE)
             out_pass(n, 0)
             features_pass(n + 1, 3)
             out_pass(n, 1)
@@ -517,8 +521,8 @@ def tile_mamba3core_t_kernel(
         square(n - 1, 1)
         scale_y(n, 3)
         invert_rms(n - 1, 0, 1)
-        regroup_y(n, SPLIT)
-        regroup_y_rest(n, SPLIT)
+        regroup_y(n, FOR_SCALAR)
+        regroup_y_gpsimd(n, FOR_GPSIMD)
         new_state(n, 0)
         tokens_pass(n, 2)
         new_state(n, 1)
@@ -534,7 +538,7 @@ def tile_mamba3core_t_kernel(
         invert_rms(n - 1, 2, 3)
         new_state(n, 2)
         store_residual(n - 2, 0, 1)
-        quantise_y(n)
+        quantise_y(n, WHOLE)
         for i in range(TILES):
             out_pass(n, i, quick_bank if i < QUICK_BANKS else out_bank)
         new_state(n, 3)

@@ -26,7 +26,7 @@ QUICK_BANKS = 3
 WHOLE = slice(0, GROUP)
 FIRST_HALF = slice(0, HALF)
 SECOND_HALF = slice(HALF, GROUP)
-SPLIT = 384
+SPLIT = 448
 FOR_SCALAR = slice(0, SPLIT)
 FOR_GPSIMD = slice(SPLIT, GROUP)
 

from contextlib import ExitStack

import concourse.masks as masks
import concourse.mybir as mybir

F32 = mybir.dt.float32
BF16 = mybir.dt.bfloat16
U32 = mybir.dt.uint32
U8 = mybir.dt.uint8
FP8X4 = mybir.dt.float8_e4m3fn_x4
ACT = mybir.ActivationFunctionType
ALU = mybir.AluOpType

P = 128
PACK = 4
D = P * PACK
TOKENS = 4 * 1024
GROUP = 512
TILES = GROUP // P
N_GROUPS = TOKENS // GROUP
EPS = 2.0 ** -23
HALF = GROUP // 2
TOKEN_BANKS = 2
OUT_BANKS = 3
QUICK_BANKS = 3
WHOLE = slice(0, GROUP)
FIRST_HALF = slice(0, HALF)
SECOND_HALF = slice(HALF, GROUP)
SPLIT = 448
FOR_SCALAR = slice(0, SPLIT)
FOR_GPSIMD = slice(SPLIT, GROUP)

FLOPS = 2 * 2 * TOKENS * D * D

ROW_B_REAL = 0
ROW_B_IMAG = 1
ROW_C_REAL = 2
ROW_C_IMAG = 3


def tile_mamba3core_t_kernel(
    tc, x, W_in, W_out, A_theta, B_real, B_imag, C_real, C_imag, norm_w, out_0, out_1, out_2
):
    nc = tc.nc

    x_groups = x.rearrange("b (h p j) k -> (b h) p j k", p=P, j=TILES)
    res_groups = out_0.rearrange("b (h p j) k -> (b h) p j k", p=P, j=TILES)
    nr_groups = out_1.rearrange("b (h p j) c d n -> (b h) p j (c d n)", p=P, j=TILES)
    ni_groups = out_2.rearrange("b (h p j) c d n -> (b h) p j (c d n)", p=P, j=TILES)

    with ExitStack() as ctx:
        ctx.enter_context(tc.manual_schedule())
        consts = ctx.enter_context(tc.tile_pool(name="consts", bufs=1))
        stage = ctx.enter_context(tc.tile_pool(name="stage", bufs=1))
        codes = ctx.enter_context(tc.tile_pool(name="codes", bufs=1))
        results = ctx.enter_context(tc.tile_pool(name="results", bufs=1))
        small = ctx.enter_context(tc.tile_pool(name="small", bufs=1))
        psum = ctx.enter_context(tc.psum_pool(name="psum", bufs=1))
        made = {}

        def rotate(pool, kind, depth, shape, dtype, align_bytes=None):
            k = made.get(kind, 0)
            made[kind] = k + 1
            tag = "%s%d" % (kind, k % depth)
            return pool.tile(shape, dtype, name=tag, tag=tag, align_bytes=align_bytes)

        def tokens_bank(shape, dtype):
            return rotate(psum, "bank_tokens", TOKEN_BANKS, shape, dtype)

        def out_bank(shape, dtype):
            return rotate(psum, "bank_out", OUT_BANKS, shape, dtype)

        def quick_bank(shape, dtype):
            return rotate(psum, "bank_quick", QUICK_BANKS, shape, dtype)

        vec_rows = consts.tile([P, D], BF16)
        nc.gpsimd.memset(vec_rows[:].bitcast(F32), 0.0)
        norm_row = consts.tile([P, D], BF16)
        nc.gpsimd.memset(norm_row[:].bitcast(F32), 0.0)
        for row, vec in (
            (ROW_B_REAL, B_real),
            (ROW_B_IMAG, B_imag),
            (ROW_C_REAL, C_real),
            (ROW_C_IMAG, C_imag),
        ):
            nc.scalar.dma_start(out=vec_rows[row : row + 1, :], in_=vec.rearrange("c d n -> (c n) d"))
        eps = consts.tile([P, 1], F32)
        nc.vector.memset(eps[:], EPS)
        table_warm = consts.tile([P, 1], F32)
        nc.scalar.activation(out=table_warm[:], in_=eps[:], func=ACT.Abs_reciprocal_sqrt)

        w_in_sb = consts.tile([P, PACK, D], BF16)
        w_out_sb = consts.tile([P, PACK, D], BF16)
        x_sb = [consts.tile([P, TILES, D], BF16, name="x_sb%d" % g) for g in range(N_GROUPS)]
        w_in_rows = W_in.rearrange("(r p) k -> p r k", p=P)
        for h in range(2):
            nc.sync.dma_start(out=w_in_sb[:, 2 * h : 2 * h + 2, :], in_=w_in_rows[:, 2 * h : 2 * h + 2, :])
        for h in range(2):
            nc.sync.dma_start(out=x_sb[0][:, 2 * h : 2 * h + 2, :], in_=x_groups[0][:, 2 * h : 2 * h + 2, :])
        nc.sync.dma_start(out=x_sb[1][:], in_=x_groups[1])
        nc.sync.dma_start(out=norm_row[0:1, :], in_=norm_w.rearrange("(o d) -> o d", o=1))
        nc.sync.dma_start(out=w_out_sb[:], in_=W_out.rearrange("(r p) k -> p r k", p=P))
        for g in range(2, N_GROUPS):
            nc.sync.dma_start(out=x_sb[g][:], in_=x_groups[g])

        ident_f32 = consts.tile([P, P], F32)
        masks.make_identity(nc, ident_f32[:])
        ident_bf16 = consts.tile([P, P], BF16)
        masks.make_identity(nc, ident_bf16[:])

        def transpose_words(planes, rows_sb, h):
            for jj in range(2):
                words = rows_sb[:, 2 * h + jj, :].bitcast(F32)
                for u in range(2):
                    nc.tensor.transpose(
                        planes[:, u, jj * P : (jj + 1) * P], words[:, u * P : (u + 1) * P], ident_f32[:]
                    )

        def interleave_words(copy, planes, grouped, h):
            copy(
                out=grouped[:].bitcast(F32)[:, h * GROUP : (h + 1) * GROUP].rearrange("p (c u) -> p c u", u=2),
                in_=planes[:].rearrange("p u c -> p c u"),
            )

        x_planes = {}
        x_grouped = {}
        x_codes = {}
        x_scales = {}

        def transpose_x(g, h):
            x_planes[(g, h)] = quick_bank([P, 2, HALF], F32)
            transpose_words(x_planes[(g, h)], x_sb[g], h)

        def interleave_x(g, h):
            if h == 0:
                x_grouped[g] = rotate(stage, "x_grouped", 2, [P, PACK * GROUP], BF16, 64)
            interleave_words(nc.scalar.copy, x_planes[(g, h)], x_grouped[g], h)

        def quantise_x(g, tokens):
            if tokens.start == 0:
                x_codes[g] = rotate(codes, "x_codes", 3, [P, GROUP], U32, 64)
                x_scales[g] = rotate(codes, "x_scales", 3, [P, GROUP], U8, 64)
            nc.vector.quantize_mx(
                out=x_codes[g][:, tokens].bitcast(FP8X4),
                scales=x_scales[g][:, tokens],
                in_=x_grouped[g][:, PACK * tokens.start : PACK * tokens.stop],
            )

        w_in_grouped = consts.tile([P, PACK * D], BF16, align_bytes=64)
        w_in_codes = consts.tile([P, D], U32, align_bytes=64)
        w_in_scales = consts.tile([P, D], U8, align_bytes=64)
        for h in range(2):
            w_in_planes = tokens_bank([P, 2, HALF], F32)
            transpose_words(w_in_planes, w_in_sb, h)
            interleave_words(nc.vector.tensor_copy, w_in_planes, w_in_grouped, h)
        nc.vector.quantize_mx(out=w_in_codes[:].bitcast(FP8X4), scales=w_in_scales[:], in_=w_in_grouped[:])

        transpose_x(0, 0)
        interleave_x(0, 0)
        quantise_x(0, FIRST_HALF)

        b_all = consts.tile([P, 2, D], F32)
        norm_w_all = consts.tile([P, D], F32)

        def spread_row(bank, rows, r, copy, out):
            picked = bank([P, D], F32)
            nc.tensor.matmul(
                picked[:], lhsT=ident_bf16[:, r : r + 1].to_broadcast([P, P]), rhs=rows[:], start=True, stop=True
            )
            copy(out=out, in_=picked[:])

        spread_row(out_bank, vec_rows, ROW_B_REAL, nc.vector.tensor_copy, b_all[:, 0, :])
        spread_row(out_bank, vec_rows, ROW_B_IMAG, nc.scalar.copy, b_all[:, 1, :])
        transpose_x(0, 1)
        interleave_x(0, 1)
        quantise_x(0, SECOND_HALF)

        vec_t = out_bank([P, PACK, P], BF16)
        for t in range(PACK):
            nc.tensor.transpose(vec_t[:, t, :], vec_rows[:, t * P : (t + 1) * P], ident_bf16[:])
        per_feature = consts.tile([P, PACK, 4], F32)
        nc.scalar.copy(out=per_feature[:], in_=vec_t[:, :, 0:4])
        cb_real = consts.tile([P, PACK], F32)
        cb_imag = consts.tile([P, PACK], F32)
        gain = consts.tile([P, PACK], F32)
        nc.gpsimd.tensor_tensor(
            out=cb_real[:], in0=per_feature[:, :, ROW_C_REAL], in1=per_feature[:, :, ROW_B_REAL], op=ALU.mult
        )
        nc.gpsimd.tensor_tensor(
            out=cb_imag[:], in0=per_feature[:, :, ROW_C_IMAG], in1=per_feature[:, :, ROW_B_IMAG], op=ALU.mult
        )
        nc.gpsimd.tensor_tensor(out=gain[:], in0=cb_real[:], in1=cb_imag[:], op=ALU.subtract)

        w_out_blocks = {}
        w_out_grouped = consts.tile([P, D, PACK], BF16, align_bytes=64)
        w_out_codes = consts.tile([P, D], U32, align_bytes=64)
        w_out_scales = consts.tile([P, D], U8, align_bytes=64)

        def transpose_w_out(r):
            w_out_blocks[r] = out_bank([P, PACK, P], BF16)
            for t in range(PACK):
                nc.tensor.transpose(w_out_blocks[r][:, t, :], w_out_sb[:, r, t * P : (t + 1) * P], ident_bf16[:])

        def interleave_w_out(copy, r):
            copy(out=w_out_grouped[:, r * P : (r + 1) * P, :], in_=w_out_blocks[r][:].rearrange("p t e -> p e t"))

        def quantise_w_out():
            nc.vector.quantize_mx(
                out=w_out_codes[:].bitcast(FP8X4),
                scales=w_out_scales[:],
                in_=w_out_grouped[:].rearrange("p e t -> p (e t)"),
            )

        xi_tokens = {}
        xi_copies = {}
        xi_features = {}
        state = {}
        y_planes = {}
        y_grouped = {}
        y_codes = {}
        y_scales = {}

        def tokens_pass(g, i):
            cols = slice(i * P, (i + 1) * P)
            xi_tokens[(g, i)] = tokens_bank([P, D], F32)
            nc.tensor.matmul_mx(
                out=xi_tokens[(g, i)][:],
                lhsT=x_codes[g][:, cols].bitcast(FP8X4),
                lhsT_scale=x_scales[g][:, cols],
                rhs=w_in_codes[:].bitcast(FP8X4),
                rhs_scale=w_in_scales[:],
                start=True,
                stop=True,
            )

        def features_pass(g, t):
            cols = slice(t * P, (t + 1) * P)
            xi_features[(g, t)] = quick_bank([P, GROUP], F32)
            nc.tensor.matmul_mx(
                out=xi_features[(g, t)][:],
                lhsT=w_in_codes[:, cols].bitcast(FP8X4),
                lhsT_scale=w_in_scales[:, cols],
                rhs=x_codes[g][:].bitcast(FP8X4),
                rhs_scale=x_scales[g][:],
                start=True,
                stop=True,
            )

        def new_state(g, i):
            if i == 0:
                state[g] = rotate(results, "state", 3, [P, 2, TILES, D], F32)
            nc.vector.tensor_tensor(
                out=state[g][:, :, i, :],
                in0=xi_tokens[(g, i)][:].unsqueeze(1).to_broadcast([P, 2, D]),
                in1=b_all[:],
                op=ALU.mult,
            )

        def copy_tokens(g, i):
            xi_copies[(g, i)] = rotate(stage, "xi_copy", 2, [P, D], F32)
            nc.scalar.copy(out=xi_copies[(g, i)][:], in_=xi_tokens[(g, i)][:])

        def new_state_from_copy(g, i):
            nc.gpsimd.tensor_tensor(
                out=state[g][:, :, i, :],
                in0=xi_copies[(g, i)][:].unsqueeze(1).to_broadcast([P, 2, D]),
                in1=b_all[:],
                op=ALU.mult,
            )

        def store_state(g, h):
            pair = slice(2 * h, 2 * h + 2)
            nc.sync.dma_start(out=nr_groups[g][:, pair, :], in_=state[g][:, 0, pair, :])
            nc.sync.dma_start(out=ni_groups[g][:, pair, :], in_=state[g][:, 1, pair, :])

        def scale_y(g, t):
            if t == 0:
                y_planes[g] = rotate(stage, "y_planes", 2, [P, PACK, GROUP], BF16)
                y_grouped[g] = rotate(stage, "y_grouped", 2, [P, GROUP, PACK], BF16, 64)
            nc.scalar.activation(
                out=y_planes[g][:, t, :], in_=xi_features[(g, t)][:], func=ACT.Copy, scale=gain[:, t : t + 1]
            )

        def regroup_y(g, tokens):
            nc.scalar.copy(
                out=y_grouped[g][:, tokens, :].rearrange("p (c i) t -> p c t i", i=4),
                in_=y_planes[g][:, :, tokens].rearrange("p t (c i) -> p c t i", i=4),
            )

        def regroup_y_gpsimd(g, tokens):
            nc.gpsimd.tensor_scalar(
                out=y_grouped[g][:, tokens, :],
                in0=y_planes[g][:, :, tokens].rearrange("p t c -> p c t"),
                scalar1=1.0,
                scalar2=0.0,
                op0=ALU.mult,
                op1=ALU.add,
            )

        def quantise_y(g, tokens):
            if tokens.start == 0:
                y_codes[g] = rotate(codes, "y_codes", 3, [P, GROUP], U32, 64)
                y_scales[g] = rotate(codes, "y_scales", 3, [P, GROUP], U8, 64)
            nc.vector.quantize_mx(
                out=y_codes[g][:, tokens].bitcast(FP8X4),
                scales=y_scales[g][:, tokens],
                in_=y_grouped[g][:, tokens, :].rearrange("p c t -> p (c t)"),
            )

        out_tokens = {}
        rstd = {}
        res = {}

        def out_pass(g, i, bank=out_bank):
            cols = slice(i * P, (i + 1) * P)
            out_tokens[(g, i)] = bank([P, D], F32)
            nc.tensor.matmul_mx(
                out=out_tokens[(g, i)][:],
                lhsT=y_codes[g][:, cols].bitcast(FP8X4),
                lhsT_scale=y_scales[g][:, cols],
                rhs=w_out_codes[:].bitcast(FP8X4),
                rhs_scale=w_out_scales[:],
                start=True,
                stop=True,
            )

        sumsq = {}

        def square(g, i):
            if i == 0:
                sumsq[g] = rotate(small, "sumsq", 2, [P, TILES], F32)
                rstd[g] = rotate(small, "rstd", 2, [P, TILES], F32)
            squares = rotate(stage, "squares", 2, [P, D], BF16)
            nc.scalar.activation(
                out=squares[:], in_=out_tokens[(g, i)][:], func=ACT.Square, accum_out=sumsq[g][:, i : i + 1]
            )

        def invert_rms(g, first, last):
            cols = slice(first, last + 1)
            nc.scalar.activation(
                out=rstd[g][:, cols],
                in_=sumsq[g][:, cols],
                func=ACT.Abs_reciprocal_sqrt,
                scale=1.0 / D,
                bias=eps[:],
            )

        def normalise(g, i):
            if g not in res:
                res[g] = rotate(results, "res", 3, [P, TILES, D], F32)
            nc.vector.scalar_tensor_tensor(
                out=res[g][:, i, :],
                in0=out_tokens[(g, i)][:],
                scalar=rstd[g][:, i : i + 1],
                in1=norm_w_all[:],
                op0=ALU.mult,
                op1=ALU.mult,
            )

        def add_residual(adder, g, first, last):
            tiles = slice(first, last + 1)
            adder.tensor_tensor(
                out=res[g][:, tiles, :], in0=res[g][:, tiles, :], in1=x_sb[g][:, tiles, :], op=ALU.add
            )

        def store_residual(g, first, last):
            tiles = slice(first, last + 1)
            nc.sync.dma_start(out=res_groups[g][:, tiles, :], in_=res[g][:, tiles, :])

        LAST = N_GROUPS - 1

        def exists(g):
            return 0 <= g < N_GROUPS

        transpose_x(1, 0)
        interleave_x(1, 0)
        tokens_pass(0, 0)
        tokens_pass(0, 1)
        transpose_x(1, 1)
        interleave_x(1, 1)
        for t in range(3):
            features_pass(0, t)
        new_state(0, 0)
        tokens_pass(0, 2)
        features_pass(0, 3)
        for t in range(PACK):
            scale_y(0, t)
        regroup_y_gpsimd(0, WHOLE)
        new_state(0, 1)
        store_state(0, 0)
        tokens_pass(0, 3)
        quantise_x(1, WHOLE)
        for r in range(3):
            transpose_w_out(r)
        for h in range(2):
            transpose_x(2, h)
        interleave_w_out(nc.scalar.copy, 0)
        interleave_w_out(nc.scalar.copy, 1)
        for h in range(2):
            interleave_x(2, h)
        new_state(0, 2)
        interleave_w_out(nc.vector.tensor_copy, 2)
        tokens_pass(1, 0)
        transpose_w_out(3)
        new_state(0, 3)
        store_state(0, 1)
        interleave_w_out(nc.vector.tensor_copy, 3)
        spread_row(quick_bank, norm_row, 0, nc.scalar.copy, norm_w_all[:])
        features_pass(1, 0)
        features_pass(1, 1)
        tokens_pass(1, 1)
        quantise_w_out()
        quantise_y(0, WHOLE)

        features_pass(1, 2)
        features_pass(1, 3)
        for t in range(PACK):
            scale_y(1, t)
        out_pass(0, 0)
        out_pass(0, 1)
        out_pass(0, 2)
        transpose_x(3, 0)
        new_state(1, 0)
        tokens_pass(1, 2)
        new_state(1, 1)
        store_state(1, 0)
        tokens_pass(1, 3)
        transpose_x(3, 1)
        square(0, 0)
        square(0, 1)
        interleave_x(3, 0)
        invert_rms(0, 0, 1)
        square(0, 2)
        regroup_y(1, FIRST_HALF)
        regroup_y_gpsimd(1, SECOND_HALF)
        new_state(1, 2)
        quantise_x(2, WHOLE)
        transpose_x(4, 0)
        tokens_pass(2, 0)
        normalise(0, 0)
        normalise(0, 1)
        new_state(1, 3)
        store_state(1, 1)
        out_pass(0, 3)
        features_pass(2, 0)
        features_pass(2, 1)
        tokens_pass(2, 1)
        interleave_x(3, 1)
        square(0, 3)
        interleave_x(4, 0)
        invert_rms(0, 2, 3)
        features_pass(2, 2)
        quantise_y(1, WHOLE)
        out_pass(1, 0)
        features_pass(2, 3)
        out_pass(1, 1)
        transpose_x(4, 1)
        out_pass(1, 2)
        normalise(0, 2)
        normalise(0, 3)
        add_residual(nc.gpsimd, 0, 2, 3)
        store_residual(0, 2, 3)
        quantise_x(3, WHOLE)

        for n in range(2, LAST):
            scale_y(n, 0)
            scale_y(n, 1)
            scale_y(n, 2)
            square(n - 1, 0)
            square(n - 1, 1)
            scale_y(n, 3)
            invert_rms(n - 1, 0, 1)
            square(n - 1, 2)
            regroup_y(n, FOR_SCALAR)
            regroup_y_gpsimd(n, FOR_GPSIMD)
            new_state(n, 0)
            tokens_pass(n, 2)
            new_state(n, 1)
            store_state(n, 0)
            add_residual(nc.gpsimd, n - 2, 0, 1)
            tokens_pass(n, 3)
            if exists(n + 3):
                transpose_x(n + 3, 0)
            normalise(n - 1, 0)
            normalise(n - 1, 1)
            new_state(n, 2)
            store_residual(n - 2, 0, 1)
            new_state(n, 3)
            store_state(n, 1)
            out_pass(n - 1, 3)
            if exists(n + 2):
                interleave_x(n + 2, 1)
            square(n - 1, 3)
            if exists(n + 3):
                interleave_x(n + 3, 0)
            invert_rms(n - 1, 2, 3)
            features_pass(n + 1, 0)
            features_pass(n + 1, 1)
            tokens_pass(n + 1, 0)
            features_pass(n + 1, 2)
            tokens_pass(n + 1, 1)
            quantise_y(n, WHOLE)
            out_pass(n, 0)
            features_pass(n + 1, 3)
            out_pass(n, 1)
            if exists(n + 3):
                transpose_x(n + 3, 1)
            out_pass(n, 2)
            normalise(n - 1, 2)
            normalise(n - 1, 3)
            add_residual(nc.gpsimd, n - 1, 2, 3)
            store_residual(n - 1, 2, 3)
            if exists(n + 2):
                quantise_x(n + 2, WHOLE)

        n = LAST
        scale_y(n, 0)
        scale_y(n, 1)
        scale_y(n, 2)
        square(n - 1, 0)
        square(n - 1, 1)
        scale_y(n, 3)
        invert_rms(n - 1, 0, 1)
        regroup_y(n, FOR_SCALAR)
        regroup_y_gpsimd(n, FOR_GPSIMD)
        new_state(n, 0)
        tokens_pass(n, 2)
        new_state(n, 1)
        store_state(n, 0)
        add_residual(nc.gpsimd, n - 2, 0, 1)
        tokens_pass(n, 3)
        out_pass(n - 1, 3)
        normalise(n - 1, 0)
        normalise(n - 1, 1)
        add_residual(nc.gpsimd, n - 1, 0, 1)
        square(n - 1, 2)
        square(n - 1, 3)
        invert_rms(n - 1, 2, 3)
        new_state(n, 2)
        store_residual(n - 2, 0, 1)
        quantise_y(n, WHOLE)
        for i in range(TILES):
            out_pass(n, i, quick_bank if i < QUICK_BANKS else out_bank)
        new_state(n, 3)
        store_state(n, 1)
        store_residual(n - 1, 0, 1)
        normalise(n - 1, 2)
        normalise(n - 1, 3)
        add_residual(nc.gpsimd, n - 1, 2, 3)
        store_residual(n - 1, 2, 3)
        square(n, 0)
        for i in range(1, TILES):
            square(n, i)
            invert_rms(n, i - 1, i - 1)
        invert_rms(n, TILES - 1, TILES - 1)
        normalise(n, 0)
        normalise(n, 1)
        normalise(n, 2)
        add_residual(nc.vector, n, 0, 1)
        store_residual(n, 0, 1)
        add_residual(nc.vector, n, 2, 2)
        store_residual(n, 2, 2)
        normalise(n, 3)
        add_residual(nc.vector, n, 3, 3)
        store_residual(n, 3, 3)
